import numpy as np
import ml_dtypes


def mxq(x, axis, fmt="e4m3"):
    dtype, down = {"e4m3": (ml_dtypes.float8_e4m3fn, 7), "e5m2": (ml_dtypes.float8_e5m2, 14)}[fmt]
    v = np.moveaxis(np.asarray(x, np.float32).astype(ml_dtypes.bfloat16).astype(np.float64), axis, -1)
    blocks = v.reshape(v.shape[:-1] + (-1, 32))
    amax = np.abs(blocks).max(-1, keepdims=True)
    byte = np.maximum(np.where(amax > 0, np.frexp(amax)[1] - 1 + 127, 0) - down, 1)
    scale = np.exp2(byte - 127.0)
    codes = (blocks / scale).astype(np.float32).astype(dtype).astype(np.float64)
    return np.moveaxis((codes * scale).reshape(v.shape), -1, axis)


WIDE = False


def mx_kscale(k):
    if not WIDE:
        return np.ones(k)
    levels = np.array([10, -10, 5, -5, 0])
    a = np.random.permutation(np.resize(levels, k // 512 * 4)).reshape(k // 512, 4)
    idx = np.arange(k)
    return np.exp2(a[idx // 512, idx % 128 // 32])


BF16 = ml_dtypes.bfloat16


def bf(x):
    return np.asarray(x, np.float32).astype(BF16)


def f64(x):
    return np.asarray(x).astype(np.float64)


B, C, GH, GW, F, D, K, T = 2, 1536, 32, 16, 512, 8192, 128, 256
N = GH * GW
EPS_NORM = 1e-12
EPS_DENOM = 1e-6


def l2norm(x, axis):
    n = np.sqrt(np.sum(x * x, axis=axis, keepdims=True))
    return x / np.maximum(n, EPS_NORM)


def sigmoid(z):
    return 1.0 / (1.0 + np.exp(-z))


def setup_inputs():
    t = mx_kscale(F)
    c = np.random.standard_normal((B, D))
    g = np.random.standard_normal((B, N))
    f = c[:, :, None] * g[:, None, :] + np.random.standard_normal((B, D, N))
    return {"f_clu": bf(f),
            "h_score": bf(np.maximum(np.random.standard_normal((B, F, N)), 0.0) * t[None, :, None]),
            "W_s2": bf(np.random.standard_normal((K, F)) * 2.5 / np.sqrt(F) / t[None, :]),
            "b_s2": bf(np.random.standard_normal(K) * 0.5),
            "burst_par": bf([5.0 + 0.25 * np.random.standard_normal(),
                             -2.5 + 0.25 * np.random.standard_normal(),
                             0.75 + 0.05 * np.random.standard_normal()])}


def reference(f_clu, h_score, W_s2, b_s2, burst_par):
    f = f64(f_clu)
    a_par, b_par, p_par = f64(burst_par)
    scores = (mxq(f64(W_s2), 1, "e4m3") @ mxq(f64(h_score), 1, "e4m3")) + f64(b_s2)[None, :, None]
    e = np.exp(scores - scores.max(axis=1, keepdims=True))
    alpha = e / e.sum(axis=1, keepdims=True)
    fq = mxq(l2norm(f, 1), 1, "e4m3")
    sim = fq.transpose(0, 2, 1) @ fq
    w = sigmoid(a_par * sim + b_par).sum(axis=2)
    pmat = alpha / (np.power(w, p_par)[:, None, :] + EPS_DENOM)
    v = mxq(f, 2, "e4m3") @ mxq(pmat, 2, "e4m3").transpose(0, 2, 1)
    return l2norm(v, 1)

@@ -1,0 +1,435 @@
+from contextlib import ExitStack
+
+import concourse.mybir as mybir
+from concourse.masks import make_identity
+
+F32 = mybir.dt.float32
+BF16 = mybir.dt.bfloat16
+U32 = mybir.dt.uint32
+U8 = mybir.dt.uint8
+FP8X4 = mybir.dt.float8_e4m3fn_x4
+ACT = mybir.ActivationFunctionType
+ALU = mybir.AluOpType
+AXIS = mybir.AxisListType
+
+IMAGES = 2
+D_FEAT = 8192
+N_PIX = 512
+K_CLU = 128
+F_HID = 512
+P = 128
+PACK = 4
+K_PASS = P * PACK
+CHUNKS = D_FEAT // K_PASS
+HALF = CHUNKS // 2
+PAIR = 2
+EPS_NORM_SQUARED = 1e-24
+EPS_DENOM = 1e-6
+ROW_TILES = 18
+AHEAD = 3
+GPSIMD_EVERY = 3
+
+FLOPS = 2 * IMAGES * (K_CLU * F_HID * N_PIX + N_PIX * D_FEAT * N_PIX + D_FEAT * N_PIX * K_CLU)
+
+
+def tile_salad_pa_k_kernel(tc, f_clu, h_score, W_s2, b_s2, burst_par, out):
+    nc = tc.nc
+    with ExitStack() as ctx:
+        const = ctx.enter_context(tc.tile_pool(name="const", bufs=1))
+        rows_pool = ctx.enter_context(tc.tile_pool(name="rows", bufs=ROW_TILES))
+        turned_pool = ctx.enter_context(tc.tile_pool(name="turned", bufs=3))
+        image_pool = ctx.enter_context(tc.tile_pool(name="image", bufs=IMAGES))
+        pass_pool = ctx.enter_context(tc.tile_pool(name="pass", bufs=3))
+        gpsimd_pool = ctx.enter_context(tc.tile_pool(name="gpsimd", bufs=2))
+        unread_pool = ctx.enter_context(tc.tile_pool(name="unread", bufs=2))
+        small = ctx.enter_context(tc.tile_pool(name="small", bufs=2))
+        sim_banks = ctx.enter_context(tc.psum_pool(name="sim_banks", bufs=PACK))
+        norm_bank = ctx.enter_context(tc.psum_pool(name="norm_bank", bufs=1))
+        banks = ctx.enter_context(tc.psum_pool(name="banks", bufs=3))
+
+        ident = const.tile([P, P], F32)
+        make_identity(nc, ident[:])
+        minus_half = const.tile([P, PACK], F32)
+        nc.vector.memset(minus_half[:], -0.5)
+        first_exp = const.tile([P, 1], F32)
+        nc.vector.memset(first_exp[:], 0.0)
+        nc.scalar.activation(out=first_exp[:], in_=first_exp[:], func=ACT.Exp)
+
+        par_bf = const.tile([P, 3], BF16)
+        nc.scalar.dma_start(out=par_bf[:], in_=burst_par.partition_broadcast(P))
+        par = const.tile([P, 3], F32)
+        nc.vector.tensor_copy(out=par[:], in_=par_bf[:])
+        exponent = const.tile([P, PACK], F32)
+        nc.vector.tensor_copy(out=exponent[:], in_=par_bf[:, 2:3].to_broadcast([P, PACK]))
+        bias = const.tile([P, K_CLU], BF16)
+        nc.scalar.dma_start(out=bias[:], in_=b_s2.partition_broadcast(P))
+        w_rows = const.tile([K_CLU, F_HID], BF16)
+        nc.scalar.dma_start(out=w_rows[:], in_=W_s2)
+
+        def load_rows(dram_rows):
+            rows = rows_pool.tile([P, PACK, N_PIX], BF16, tag="rows")
+            nc.sync.dma_start(out=rows[:], in_=dram_rows.rearrange("(p j) n -> p j n", j=PACK))
+            return rows
+
+        def columns_by_slot(grouped):
+            return grouped[:].rearrange("p (t q) j -> p t q j", t=PACK)
+
+        def pixels_by_slot(rows):
+            return rows[:].rearrange("p j (q t) -> p t q j", t=PACK)
+
+        def quantise(grouped_columns, codes, scales):
+            nc.vector.quantize_mx(
+                out=codes.bitcast(FP8X4),
+                scales=scales,
+                in_=grouped_columns.rearrange("p c j -> p (c j)"),
+            )
+
+        def quantise_pass(grouped):
+            codes = pass_pool.tile([P, N_PIX], U32, tag="codes", align_bytes=64)
+            scales = pass_pool.tile([P, N_PIX], U8, tag="scales", align_bytes=64)
+            quantise(grouped[:], codes[:], scales[:])
+            return codes, scales
+
+        def inverse_root(squares, width):
+            floored = small.tile([P, width], F32, tag="floored%d" % width)
+            nc.vector.tensor_scalar_max(out=floored[:], in0=squares[:], scalar1=EPS_NORM_SQUARED)
+            inverse = small.tile([P, width], F32, tag="inverse%d" % width)
+            nc.gpsimd.tensor_tensor(
+                out=inverse[:], in0=floored[:], in1=minus_half[:, 0:width], op=ALU.pow
+            )
+            return inverse
+
+        def spread_over_partitions(bank_columns, column):
+            nc.tensor.matmul(
+                out=bank_columns, lhsT=column.to_broadcast([P, P]), rhs=ident[:], start=True, stop=True
+            )
+
+        w_words = w_rows[:].bitcast(F32).rearrange("k (q u) -> k u q", u=2)
+        w_turned = banks.tile([P, 2, K_CLU], F32, tag="bank")
+        for u in range(2):
+            nc.tensor.transpose(w_turned[:, u, :], w_words[:, u, :], ident[:])
+        w_grouped = const.tile([P, K_CLU, PACK], BF16, align_bytes=64)
+        nc.vector.tensor_copy(
+            out=w_grouped[:].bitcast(F32), in_=w_turned[:].rearrange("q u k -> q k u")
+        )
+        w_codes = const.tile([P, K_CLU], U32, align_bytes=64)
+        w_scales = const.tile([P, K_CLU], U8, align_bytes=64)
+        quantise(w_grouped[:], w_codes[:], w_scales[:])
+
+        def new_image(i):
+            return {
+                "index": i,
+                "rows": [],
+                "turned": [],
+                "scaled": [],
+                "fT_codes": image_pool.tile(
+                    [P, D_FEAT], U32, name="fT_codes", tag="fT_codes", align_bytes=64
+                ),
+                "fT_scales": image_pool.tile(
+                    [P, D_FEAT], U8, name="fT_scales", tag="fT_scales", align_bytes=64
+                ),
+                "pixel_squares": small.tile(
+                    [P, PACK, CHUNKS // PAIR], F32, name="pixel_squares", tag="pixel_squares"
+                ),
+                "cluster_squares": small.tile(
+                    [P, CHUNKS], F32, name="cluster_squares", tag="cluster_squares"
+                ),
+            }
+
+        def load_chunk(im, c):
+            im["rows"].append(load_rows(f_clu[im["index"], c * K_PASS : (c + 1) * K_PASS, :]))
+
+        def transpose_chunk(im, c):
+            words = im["rows"][c][:].bitcast(F32).rearrange("p j (q u) -> p j u q", u=2)
+            two_banks = []
+            for half in range(2):
+                bank = banks.tile([P, 2, 2, P], F32, name="turned_bank", tag="bank")
+                for jj in range(2):
+                    for u in range(2):
+                        nc.tensor.transpose(bank[:, jj, u, :], words[:, 2 * half + jj, u, :], ident[:])
+                two_banks.append(bank)
+            return two_banks
+
+        def empty_banks(im, c, two_banks, copies):
+            if c % PAIR == 0:
+                im["turned"].append(
+                    turned_pool.tile(
+                        [P, PAIR * K_PASS, PACK], BF16, name="turned", tag="turned", align_bytes=64
+                    )
+                )
+            turned_words = im["turned"][c // PAIR][:].bitcast(F32)
+            for half in range(2):
+                first = (c % PAIR) * K_PASS + half * 2 * P
+                copies[half](
+                    out=turned_words[:, first : first + 2 * P, :].rearrange(
+                        "q (jj p) u -> q jj p u", jj=2
+                    ),
+                    in_=two_banks[half][:].rearrange("q jj u p -> q jj p u"),
+                )
+
+        def quantise_turned(im, c):
+            columns = slice(c * K_PASS, (c + 1) * K_PASS)
+            first = (c % PAIR) * K_PASS
+            quantise(
+                im["turned"][c // PAIR][:, first : first + K_PASS, :],
+                im["fT_codes"][:, columns],
+                im["fT_scales"][:, columns],
+            )
+
+        def square_pair(im, pair, slots):
+            for t in slots:
+                unread = unread_pool.tile([P, PAIR * K_PASS], BF16, tag="squares")
+                nc.scalar.activation(
+                    out=unread[:],
+                    in_=im["turned"][pair][:, :, t],
+                    func=ACT.Square,
+                    accum_out=im["pixel_squares"][:, t, pair : pair + 1],
+                )
+
+        def soft_assignment(im):
+            h_rows = load_rows(h_score[im["index"]])
+            h_grouped = pass_pool.tile([P, N_PIX, PACK], BF16, tag="grouped", align_bytes=64)
+            nc.vector.tensor_copy(out=columns_by_slot(h_grouped), in_=pixels_by_slot(h_rows))
+            h_codes, h_scales = quantise_pass(h_grouped)
+            product = banks.tile([P, PACK, K_CLU], F32, tag="bank")
+            for t in range(PACK):
+                nc.tensor.matmul_mx(
+                    out=product[:, t, :],
+                    lhsT=h_codes[:, t * P : (t + 1) * P].bitcast(FP8X4),
+                    lhsT_scale=h_scales[:, t * P : (t + 1) * P],
+                    rhs=w_codes[:].bitcast(FP8X4),
+                    rhs_scale=w_scales[:],
+                    start=True,
+                    stop=True,
+                )
+            expo = image_pool.tile([P, PACK, K_CLU], F32, tag="expo")
+            nc.vector.tensor_tensor(
+                out=expo[:],
+                in0=product[:],
+                in1=bias[:].unsqueeze(1).to_broadcast([P, PACK, K_CLU]),
+                op=ALU.add,
+            )
+            top = small.tile([P, PACK], F32, tag="top")
+            nc.vector.tensor_reduce(out=top[:], in_=expo[:], axis=AXIS.X, op=ALU.max)
+            minus_top = small.tile([P, PACK], F32, tag="minus_top")
+            nc.vector.tensor_scalar_mul(out=minus_top[:], in0=top[:], scalar1=-1.0)
+            expo_sum = image_pool.tile([P, PACK], F32, tag="expo_sum")
+            for t in range(PACK):
+                nc.scalar.activation(
+                    out=expo[:, t, :],
+                    in_=expo[:, t, :],
+                    func=ACT.Exp,
+                    bias=minus_top[:, t : t + 1],
+                    accum_out=expo_sum[:, t : t + 1],
+                )
+            im["expo"] = expo
+            im["expo_sum"] = expo_sum
+
+        def pixel_norms(im):
+            squared_norm = small.tile([P, PACK], F32, tag="squared_norm")
+            nc.vector.tensor_reduce(
+                out=squared_norm[:], in_=im["pixel_squares"][:], axis=AXIS.X, op=ALU.add
+            )
+            inverse_norm = inverse_root(squared_norm, PACK)
+            spread = norm_bank.tile([P, PACK, P], F32, tag="spread")
+            for t in range(PACK):
+                spread_over_partitions(spread[:, t, :], inverse_norm[:, t : t + 1])
+            spread_copy = const.tile([P, PACK, P], F32, tag="spread_copy")
+            nc.vector.tensor_copy(out=spread_copy[:], in_=spread[:])
+            im["spread"] = spread
+            im["spread_copy"] = spread_copy
+
+        def scale_chunk(im, c):
+            if c % GPSIMD_EVERY == GPSIMD_EVERY - 1:
+                grouped = gpsimd_pool.tile([P, N_PIX, PACK], BF16, tag="grouped", align_bytes=64)
+                engine, norms = nc.gpsimd, im["spread_copy"]
+            else:
+                grouped = pass_pool.tile([P, N_PIX, PACK], BF16, tag="grouped", align_bytes=64)
+                engine, norms = nc.vector, im["spread"]
+            engine.tensor_tensor(
+                out=columns_by_slot(grouped),
+                in0=pixels_by_slot(im["rows"][c]),
+                in1=norms[:].unsqueeze(3).to_broadcast([P, PACK, P, PACK]),
+                op=ALU.mult,
+            )
+            im["scaled"].append(grouped)
+
+        def similarity_pass(im, c):
+            if c == 0:
+                im["sim"] = [
+                    sim_banks.tile([P, N_PIX], F32, name="sim%d" % t, tag="sim") for t in range(PACK)
+                ]
+            fn_codes, fn_scales = quantise_pass(im["scaled"][c])
+            for t in range(PACK):
+                nc.tensor.matmul_mx(
+                    out=im["sim"][t][:],
+                    lhsT=fn_codes[:, t * P : (t + 1) * P].bitcast(FP8X4),
+                    lhsT_scale=fn_scales[:, t * P : (t + 1) * P],
+                    rhs=fn_codes[:].bitcast(FP8X4),
+                    rhs_scale=fn_scales[:],
+                    start=(c == 0),
+                    stop=(c == CHUNKS - 1),
+                )
+
+        def burst_weights(im):
+            w = small.tile([P, PACK], F32, tag="w")
+            for t in range(PACK):
+                unread = unread_pool.tile([P, N_PIX], BF16, tag="bank_wide")
+                nc.scalar.activation(
+                    out=unread[:],
+                    in_=im["sim"][t][:],
+                    func=ACT.Sigmoid,
+                    scale=par[:, 0:1],
+                    bias=par[:, 1:2],
+                    accum_out=w[:, t : t + 1],
+                )
+            w_power = small.tile([P, PACK], F32, tag="w_power")
+            nc.gpsimd.tensor_tensor(out=w_power[:], in0=w[:], in1=exponent[:], op=ALU.pow)
+            im["w_power"] = w_power
+
+        def weighted_assignment(im):
+            divisor = small.tile([P, PACK], F32, tag="divisor")
+            nc.vector.tensor_scalar_add(out=divisor[:], in0=im["w_power"][:], scalar1=EPS_DENOM)
+            nc.vector.tensor_mul(out=divisor[:], in0=divisor[:], in1=im["expo_sum"][:])
+            share = small.tile([P, PACK], F32, tag="share")
+            nc.vector.reciprocal(out=share[:], in_=divisor[:])
+            pm_grouped = small.tile([P, K_CLU, PACK], BF16, tag="pm_grouped", align_bytes=64)
+            nc.vector.tensor_tensor(
+                out=pm_grouped[:],
+                in0=im["expo"][:].rearrange("q t k -> q k t"),
+                in1=share[:].unsqueeze(1).to_broadcast([P, K_CLU, PACK]),
+                op=ALU.mult,
+            )
+            pm_codes = image_pool.tile([P, K_CLU], U32, tag="pm_codes", align_bytes=64)
+            pm_scales = image_pool.tile([P, K_CLU], U8, tag="pm_scales", align_bytes=64)
+            quantise(pm_grouped[:], pm_codes[:], pm_scales[:])
+            im["pm_codes"] = pm_codes
+            im["pm_scales"] = pm_scales
+
+        def square_aggregate(im, c):
+            columns = slice(c * K_PASS, (c + 1) * K_PASS)
+            v_turned = banks.tile([P, K_PASS], F32, tag="bank")
+            nc.tensor.matmul_mx(
+                out=v_turned[:],
+                lhsT=im["pm_codes"][:].bitcast(FP8X4),
+                lhsT_scale=im["pm_scales"][:],
+                rhs=im["fT_codes"][:, columns].bitcast(FP8X4),
+                rhs_scale=im["fT_scales"][:, columns],
+                start=True,
+                stop=True,
+            )
+            unread = unread_pool.tile([P, K_PASS], BF16, tag="bank_wide")
+            nc.scalar.activation(
+                out=unread[:],
+                in_=v_turned[:],
+                func=ACT.Square,
+                accum_out=im["cluster_squares"][:, c : c + 1],
+            )
+
+        def cluster_norms(im):
+            squared_norm = small.tile([P, 1], F32, tag="v_squared_norm")
+            nc.vector.tensor_reduce(
+                out=squared_norm[:], in_=im["cluster_squares"][:], axis=AXIS.X, op=ALU.add
+            )
+            inverse_norm = inverse_root(squared_norm, 1)
+            spread_bank = banks.tile([P, K_CLU], F32, tag="bank")
+            spread_over_partitions(spread_bank[:], inverse_norm[:, 0:1])
+            im["v_spread_bank"] = spread_bank
+
+        def fetch_cluster_norms(im):
+            v_spread = small.tile([P, K_CLU], F32, tag="v_spread")
+            nc.vector.tensor_copy(out=v_spread[:], in_=im["v_spread_bank"][:])
+            im["v_spread"] = v_spread
+
+        def output_chunk(im, c):
+            v = banks.tile([P, PACK, K_CLU], F32, tag="bank")
+            for j in range(PACK):
+                columns = slice(c * K_PASS + j * P, c * K_PASS + (j + 1) * P)
+                nc.tensor.matmul_mx(
+                    out=v[:, j, :],
+                    lhsT=im["fT_codes"][:, columns].bitcast(FP8X4),
+                    lhsT_scale=im["fT_scales"][:, columns],
+                    rhs=im["pm_codes"][:].bitcast(FP8X4),
+                    rhs_scale=im["pm_scales"][:],
+                    start=True,
+                    stop=True,
+                )
+            normed = rows_pool.tile([P, PACK, K_CLU], F32, tag="rows")
+            nc.vector.tensor_tensor(
+                out=normed[:],
+                in0=v[:],
+                in1=im["v_spread"][:].unsqueeze(1).to_broadcast([P, PACK, K_CLU]),
+                op=ALU.mult,
+            )
+            nc.sync.dma_start(
+                out=out[im["index"], c * K_PASS : (c + 1) * K_PASS, :].rearrange(
+                    "(p j) k -> p j k", j=PACK
+                ),
+                in_=normed[:],
+            )
+
+        image0 = new_image(0)
+        image1 = new_image(1)
+
+        for c in range(CHUNKS):
+            load_chunk(image0, c)
+        for c in range(CHUNKS):
+            empty_banks(
+                image0, c, transpose_chunk(image0, c), (nc.vector.tensor_copy, nc.vector.tensor_copy)
+            )
+            if c >= 1:
+                quantise_turned(image0, c - 1)
+            if c % PAIR == PAIR - 1:
+                square_pair(image0, c // PAIR, range(PACK))
+        quantise_turned(image0, CHUNKS - 1)
+        soft_assignment(image0)
+        soft_assignment(image1)
+        pixel_norms(image0)
+
+        scale_chunk(image0, 0)
+        for c in range(AHEAD):
+            load_chunk(image1, c)
+        two_banks = transpose_chunk(image1, 0)
+        for c in range(CHUNKS):
+            if c + 1 < CHUNKS:
+                scale_chunk(image0, c + 1)
+            if c + AHEAD < CHUNKS:
+                load_chunk(image1, c + AHEAD)
+            empty_banks(image1, c, two_banks, (nc.scalar.copy, nc.vector.tensor_copy))
+            if c + 1 < CHUNKS:
+                two_banks = transpose_chunk(image1, c + 1)
+            similarity_pass(image0, c)
+            if c >= 1:
+                quantise_turned(image1, c - 1)
+            if c >= PAIR:
+                square_pair(image1, c // PAIR - 1, (2 * (c % PAIR), 2 * (c % PAIR) + 1))
+        quantise_turned(image1, CHUNKS - 1)
+        square_pair(image1, CHUNKS // PAIR - 1, range(PACK))
+        pixel_norms(image1)
+        burst_weights(image0)
+
+        scale_chunk(image1, 0)
+        weighted_assignment(image0)
+        for c in range(CHUNKS):
+            if c + 1 < CHUNKS:
+                scale_chunk(image1, c + 1)
+            similarity_pass(image1, c)
+            if c < HALF:
+                square_aggregate(image0, 2 * c)
+                square_aggregate(image0, 2 * c + 1)
+            if c == HALF:
+                cluster_norms(image0)
+
+        burst_weights(image1)
+        fetch_cluster_norms(image0)
+        for c in range(HALF):
+            output_chunk(image0, c)
+        weighted_assignment(image1)
+        for c in range(CHUNKS):
+            square_aggregate(image1, c)
+            if c < HALF:
+                output_chunk(image0, HALF + c)
+        cluster_norms(image1)
+        fetch_cluster_norms(image1)
+        for c in range(CHUNKS):
+            output_chunk(image1, c)

@@ -27,7 +27,6 @@ EPS_NORM_SQUARED = 1e-24
 EPS_DENOM = 1e-6
 ROW_TILES = 18
 AHEAD = 3
-GPSIMD_EVERY = 3
 
 FLOPS = 2 * IMAGES * (K_CLU * F_HID * N_PIX + N_PIX * D_FEAT * N_PIX + D_FEAT * N_PIX * K_CLU)
 
@@ -40,7 +39,6 @@ def tile_salad_pa_k_kernel(tc, f_clu, h_score, W_s2, b_s2, burst_par, out):
         turned_pool = ctx.enter_context(tc.tile_pool(name="turned", bufs=3))
         image_pool = ctx.enter_context(tc.tile_pool(name="image", bufs=IMAGES))
         pass_pool = ctx.enter_context(tc.tile_pool(name="pass", bufs=3))
-        gpsimd_pool = ctx.enter_context(tc.tile_pool(name="gpsimd", bufs=2))
         unread_pool = ctx.enter_context(tc.tile_pool(name="unread", bufs=2))
         small = ctx.enter_context(tc.tile_pool(name="small", bufs=2))
         sim_banks = ctx.enter_context(tc.psum_pool(name="sim_banks", bufs=PACK))
@@ -234,22 +232,14 @@ def tile_salad_pa_k_kernel(tc, f_clu, h_score, W_s2, b_s2, burst_par, out):
             spread = norm_bank.tile([P, PACK, P], F32, tag="spread")
             for t in range(PACK):
                 spread_over_partitions(spread[:, t, :], inverse_norm[:, t : t + 1])
-            spread_copy = const.tile([P, PACK, P], F32, tag="spread_copy")
-            nc.vector.tensor_copy(out=spread_copy[:], in_=spread[:])
             im["spread"] = spread
-            im["spread_copy"] = spread_copy
 
         def scale_chunk(im, c):
-            if c % GPSIMD_EVERY == GPSIMD_EVERY - 1:
-                grouped = gpsimd_pool.tile([P, N_PIX, PACK], BF16, tag="grouped", align_bytes=64)
-                engine, norms = nc.gpsimd, im["spread_copy"]
-            else:
-                grouped = pass_pool.tile([P, N_PIX, PACK], BF16, tag="grouped", align_bytes=64)
-                engine, norms = nc.vector, im["spread"]
-            engine.tensor_tensor(
+            grouped = pass_pool.tile([P, N_PIX, PACK], BF16, tag="grouped", align_bytes=64)
+            nc.vector.tensor_tensor(
                 out=columns_by_slot(grouped),
                 in0=pixels_by_slot(im["rows"][c]),
-                in1=norms[:].unsqueeze(3).to_broadcast([P, PACK, P, PACK]),
+                in1=im["spread"][:].unsqueeze(3).to_broadcast([P, PACK, P, PACK]),
                 op=ALU.mult,
             )
             im["scaled"].append(grouped)

@@ -70,10 +70,10 @@ def tile_salad_pa_k_kernel(tc, f_clu, h_score, W_s2, b_s2, burst_par, out):
             return rows
 
         def columns_by_slot(grouped):
-            return grouped[:].rearrange("p (t q) j -> p t q j", t=PACK)
+            return grouped[:].rearrange("p (t q) j -> p q j t", t=PACK)
 
         def pixels_by_slot(rows):
-            return rows[:].rearrange("p j (q t) -> p t q j", t=PACK)
+            return rows[:].rearrange("p j (q t) -> p q j t", t=PACK)
 
         def quantise(grouped_columns, codes, scales):
             nc.vector.quantize_mx(
@@ -229,9 +229,11 @@ def tile_salad_pa_k_kernel(tc, f_clu, h_score, W_s2, b_s2, burst_par, out):
                 out=squared_norm[:], in_=im["pixel_squares"][:], axis=AXIS.X, op=ALU.add
             )
             inverse_norm = inverse_root(squared_norm, PACK)
-            spread = norm_bank.tile([P, PACK, P], F32, tag="spread")
+            spread_bank = norm_bank.tile([P, PACK, P], F32, tag="spread_bank")
             for t in range(PACK):
-                spread_over_partitions(spread[:, t, :], inverse_norm[:, t : t + 1])
+                spread_over_partitions(spread_bank[:, t, :], inverse_norm[:, t : t + 1])
+            spread = const.tile([P, P, PACK], F32, tag="spread")
+            nc.vector.tensor_copy(out=spread[:], in_=spread_bank[:].rearrange("p t q -> p q t"))
             im["spread"] = spread
 
         def scale_chunk(im, c):
@@ -239,7 +241,7 @@ def tile_salad_pa_k_kernel(tc, f_clu, h_score, W_s2, b_s2, burst_par, out):
             nc.vector.tensor_tensor(
                 out=columns_by_slot(grouped),
                 in0=pixels_by_slot(im["rows"][c]),
-                in1=im["spread"][:].unsqueeze(3).to_broadcast([P, PACK, P, PACK]),
+                in1=im["spread"][:].unsqueeze(2).to_broadcast([P, P, PACK, PACK]),
                 op=ALU.mult,
             )
             im["scaled"].append(grouped)

@@ -26,7 +26,7 @@ PAIR = 2
 EPS_NORM_SQUARED = 1e-24
 EPS_DENOM = 1e-6
 ROW_TILES = 18
-AHEAD = 3
+ROUND = 3
 
 FLOPS = 2 * IMAGES * (K_CLU * F_HID * N_PIX + N_PIX * D_FEAT * N_PIX + D_FEAT * N_PIX * K_CLU)
 
@@ -39,6 +39,7 @@ def tile_salad_pa_k_kernel(tc, f_clu, h_score, W_s2, b_s2, burst_par, out):
         turned_pool = ctx.enter_context(tc.tile_pool(name="turned", bufs=3))
         image_pool = ctx.enter_context(tc.tile_pool(name="image", bufs=IMAGES))
         pass_pool = ctx.enter_context(tc.tile_pool(name="pass", bufs=3))
+        gpsimd_pool = ctx.enter_context(tc.tile_pool(name="gpsimd", bufs=1))
         unread_pool = ctx.enter_context(tc.tile_pool(name="unread", bufs=2))
         small = ctx.enter_context(tc.tile_pool(name="small", bufs=2))
         sim_banks = ctx.enter_context(tc.psum_pool(name="sim_banks", bufs=PACK))
@@ -119,7 +120,7 @@ def tile_salad_pa_k_kernel(tc, f_clu, h_score, W_s2, b_s2, burst_par, out):
                 "index": i,
                 "rows": [],
                 "turned": [],
-                "scaled": [],
+                "scaled": {},
                 "fT_codes": image_pool.tile(
                     [P, D_FEAT], U32, name="fT_codes", tag="fT_codes", align_bytes=64
                 ),
@@ -229,22 +230,31 @@ def tile_salad_pa_k_kernel(tc, f_clu, h_score, W_s2, b_s2, burst_par, out):
                 out=squared_norm[:], in_=im["pixel_squares"][:], axis=AXIS.X, op=ALU.add
             )
             inverse_norm = inverse_root(squared_norm, PACK)
-            spread_bank = norm_bank.tile([P, PACK, P], F32, tag="spread_bank")
+            spread = norm_bank.tile([P, P, PACK], F32, tag="spread")
             for t in range(PACK):
-                spread_over_partitions(spread_bank[:, t, :], inverse_norm[:, t : t + 1])
-            spread = const.tile([P, P, PACK], F32, tag="spread")
-            nc.vector.tensor_copy(out=spread[:], in_=spread_bank[:].rearrange("p t q -> p q t"))
+                spread_over_partitions(spread[:, :, t], inverse_norm[:, t : t + 1])
+            spread_copy = const.tile([P, P, PACK], F32, tag="spread_copy")
+            nc.vector.tensor_copy(out=spread_copy[:], in_=spread[:])
             im["spread"] = spread
+            im["spread_copy"] = spread_copy
+
+        def on_gpsimd(c):
+            return c % ROUND == ROUND - 1
 
         def scale_chunk(im, c):
-            grouped = pass_pool.tile([P, N_PIX, PACK], BF16, tag="grouped", align_bytes=64)
-            nc.vector.tensor_tensor(
+            if on_gpsimd(c):
+                grouped = gpsimd_pool.tile([P, N_PIX, PACK], BF16, tag="grouped", align_bytes=64)
+                engine, norms = nc.gpsimd, im["spread_copy"]
+            else:
+                grouped = pass_pool.tile([P, N_PIX, PACK], BF16, tag="grouped", align_bytes=64)
+                engine, norms = nc.vector, im["spread"]
+            engine.tensor_tensor(
                 out=columns_by_slot(grouped),
                 in0=pixels_by_slot(im["rows"][c]),
-                in1=im["spread"][:].unsqueeze(2).to_broadcast([P, P, PACK, PACK]),
+                in1=norms[:].unsqueeze(2).to_broadcast([P, P, PACK, PACK]),
                 op=ALU.mult,
             )
-            im["scaled"].append(grouped)
+            im["scaled"][c] = grouped
 
         def similarity_pass(im, c):
             if c == 0:
@@ -378,38 +388,55 @@ def tile_salad_pa_k_kernel(tc, f_clu, h_score, W_s2, b_s2, burst_par, out):
         soft_assignment(image1)
         pixel_norms(image0)
 
-        scale_chunk(image0, 0)
-        for c in range(AHEAD):
-            load_chunk(image1, c)
+
+        def load_next_chunk_of_image1():
+            if len(image1["rows"]) < CHUNKS:
+                load_chunk(image1, len(image1["rows"]))
+
+        load_next_chunk_of_image1()
+        load_next_chunk_of_image1()
+        scale_chunk(image0, ROUND - 1)
+        load_next_chunk_of_image1()
         two_banks = transpose_chunk(image1, 0)
-        for c in range(CHUNKS):
-            if c + 1 < CHUNKS:
-                scale_chunk(image0, c + 1)
-            if c + AHEAD < CHUNKS:
-                load_chunk(image1, c + AHEAD)
-            empty_banks(image1, c, two_banks, (nc.scalar.copy, nc.vector.tensor_copy))
-            if c + 1 < CHUNKS:
-                two_banks = transpose_chunk(image1, c + 1)
-            similarity_pass(image0, c)
-            if c >= 1:
-                quantise_turned(image1, c - 1)
-            if c >= PAIR:
-                square_pair(image1, c // PAIR - 1, (2 * (c % PAIR), 2 * (c % PAIR) + 1))
-        quantise_turned(image1, CHUNKS - 1)
+        for first in range(0, CHUNKS, ROUND):
+            members = range(first, min(first + ROUND, CHUNKS))
+            for c in members:
+                if not on_gpsimd(c):
+                    scale_chunk(image0, c)
+                    load_next_chunk_of_image1()
+                empty_banks(image1, c, two_banks, (nc.scalar.copy, nc.vector.tensor_copy))
+                if c + 1 < CHUNKS:
+                    two_banks = transpose_chunk(image1, c + 1)
+                if c >= PAIR:
+                    square_pair(image1, c // PAIR - 1, (2 * (c % PAIR), 2 * (c % PAIR) + 1))
+            for c in members:
+                quantise_turned(image1, c)
+            for c in members:
+                similarity_pass(image0, c)
+            if first + 2 * ROUND - 1 < CHUNKS:
+                scale_chunk(image0, first + 2 * ROUND - 1)
+                load_next_chunk_of_image1()
         square_pair(image1, CHUNKS // PAIR - 1, range(PACK))
         pixel_norms(image1)
         burst_weights(image0)
 
-        scale_chunk(image1, 0)
-        weighted_assignment(image0)
-        for c in range(CHUNKS):
-            if c + 1 < CHUNKS:
-                scale_chunk(image1, c + 1)
-            similarity_pass(image1, c)
-            if c < HALF:
-                square_aggregate(image0, 2 * c)
-                square_aggregate(image0, 2 * c + 1)
-            if c == HALF:
+        scale_chunk(image1, ROUND - 1)
+        for first in range(0, CHUNKS, ROUND):
+            members = range(first, min(first + ROUND, CHUNKS))
+            for c in members:
+                if not on_gpsimd(c):
+                    scale_chunk(image1, c)
+            if first == 0:
+                weighted_assignment(image0)
+            for c in members:
+                similarity_pass(image1, c)
+            if first + 2 * ROUND - 1 < CHUNKS:
+                scale_chunk(image1, first + 2 * ROUND - 1)
+            for c in members:
+                if c < HALF:
+                    square_aggregate(image0, 2 * c)
+                    square_aggregate(image0, 2 * c + 1)
+            if HALF - 1 + ROUND in members:
                 cluster_norms(image0)
 
         burst_weights(image1)

@@ -26,6 +26,8 @@ PAIR = 2
 EPS_NORM_SQUARED = 1e-24
 EPS_DENOM = 1e-6
 ROW_TILES = 18
+EARLY = 4
+LAG = 2
 ROUND = 3
 
 FLOPS = 2 * IMAGES * (K_CLU * F_HID * N_PIX + N_PIX * D_FEAT * N_PIX + D_FEAT * N_PIX * K_CLU)
@@ -98,10 +100,14 @@ def tile_salad_pa_k_kernel(tc, f_clu, h_score, W_s2, b_s2, burst_par, out):
             )
             return inverse
 
-        def spread_over_partitions(bank_columns, column):
-            nc.tensor.matmul(
-                out=bank_columns, lhsT=column.to_broadcast([P, P]), rhs=ident[:], start=True, stop=True
+        def spread_over_partitions(bank_views, per_partition):
+            width = len(bank_views)
+            repeated = const.tile([P, width, P], F32, tag="repeated%d" % width)
+            nc.vector.tensor_copy(
+                out=repeated[:], in_=per_partition[:].unsqueeze(2).to_broadcast([P, width, P])
             )
+            for k in range(width):
+                nc.tensor.transpose(bank_views[k], repeated[:, k, :], ident[:])
 
         w_words = w_rows[:].bitcast(F32).rearrange("k (q u) -> k u q", u=2)
         w_turned = banks.tile([P, 2, K_CLU], F32, tag="bank")
@@ -126,9 +132,6 @@ def tile_salad_pa_k_kernel(tc, f_clu, h_score, W_s2, b_s2, burst_par, out):
                 ),
                 "fT_scales": image_pool.tile(
                     [P, D_FEAT], U8, name="fT_scales", tag="fT_scales", align_bytes=64
-                ),
-                "pixel_squares": small.tile(
-                    [P, PACK, CHUNKS // PAIR], F32, name="pixel_squares", tag="pixel_squares"
                 ),
                 "cluster_squares": small.tile(
                     [P, CHUNKS], F32, name="cluster_squares", tag="cluster_squares"
@@ -185,8 +188,11 @@ def tile_salad_pa_k_kernel(tc, f_clu, h_score, W_s2, b_s2, burst_par, out):
                     accum_out=im["pixel_squares"][:, t, pair : pair + 1],
                 )
 
+        def load_hidden(im):
+            im["h_rows"] = load_rows(h_score[im["index"]])
+
         def soft_assignment(im):
-            h_rows = load_rows(h_score[im["index"]])
+            h_rows = im["h_rows"]
             h_grouped = pass_pool.tile([P, N_PIX, PACK], BF16, tag="grouped", align_bytes=64)
             nc.vector.tensor_copy(out=columns_by_slot(h_grouped), in_=pixels_by_slot(h_rows))
             h_codes, h_scales = quantise_pass(h_grouped)
@@ -224,16 +230,39 @@ def tile_salad_pa_k_kernel(tc, f_clu, h_score, W_s2, b_s2, burst_par, out):
             im["expo"] = expo
             im["expo_sum"] = expo_sum
 
-        def pixel_norms(im):
+        def add_to_gram(gram, rows, first, last):
+            for j in range(PACK):
+                for m in range(PACK):
+                    block = rows[:, j, m * P : (m + 1) * P]
+                    nc.tensor.matmul(
+                        out=gram[m][:],
+                        lhsT=block,
+                        rhs=block,
+                        start=(first and j == 0),
+                        stop=(last and j == PACK - 1),
+                    )
+
+        def diagonals(gram):
+            on_diagonal = const.tile([P, PACK, P], F32)
+            for m in range(PACK):
+                nc.vector.tensor_tensor(
+                    out=on_diagonal[:, m, :], in0=gram[m][:], in1=ident[:], op=ALU.mult
+                )
+            squared_norm = small.tile([P, PACK], F32, tag="squared_norm")
+            nc.vector.tensor_reduce(out=squared_norm[:], in_=on_diagonal[:], axis=AXIS.X, op=ALU.add)
+            return squared_norm
+
+        def summed_squares(im):
             squared_norm = small.tile([P, PACK], F32, tag="squared_norm")
             nc.vector.tensor_reduce(
                 out=squared_norm[:], in_=im["pixel_squares"][:], axis=AXIS.X, op=ALU.add
             )
-            inverse_norm = inverse_root(squared_norm, PACK)
-            spread = norm_bank.tile([P, P, PACK], F32, tag="spread")
-            for t in range(PACK):
-                spread_over_partitions(spread[:, :, t], inverse_norm[:, t : t + 1])
-            spread_copy = const.tile([P, P, PACK], F32, tag="spread_copy")
+            return squared_norm
+
+        def spread_pixel_norms(im, inverse_norm, pixels_of_column):
+            spread = norm_bank.tile([P, N_PIX], F32, tag="spread")
+            spread_over_partitions([pixels_of_column(spread, k) for k in range(PACK)], inverse_norm)
+            spread_copy = const.tile([P, N_PIX], F32, tag="spread_copy")
             nc.vector.tensor_copy(out=spread_copy[:], in_=spread[:])
             im["spread"] = spread
             im["spread_copy"] = spread_copy
@@ -251,7 +280,10 @@ def tile_salad_pa_k_kernel(tc, f_clu, h_score, W_s2, b_s2, burst_par, out):
             engine.tensor_tensor(
                 out=columns_by_slot(grouped),
                 in0=pixels_by_slot(im["rows"][c]),
-                in1=norms[:].unsqueeze(2).to_broadcast([P, P, PACK, PACK]),
+                in1=norms[:]
+                .rearrange("p (q t) -> p q t", t=PACK)
+                .unsqueeze(2)
+                .to_broadcast([P, P, PACK, PACK]),
                 op=ALU.mult,
             )
             im["scaled"][c] = grouped
@@ -335,7 +367,7 @@ def tile_salad_pa_k_kernel(tc, f_clu, h_score, W_s2, b_s2, burst_par, out):
             )
             inverse_norm = inverse_root(squared_norm, 1)
             spread_bank = banks.tile([P, K_CLU], F32, tag="bank")
-            spread_over_partitions(spread_bank[:], inverse_norm[:, 0:1])
+            spread_over_partitions([spread_bank[:]], inverse_norm)
             im["v_spread_bank"] = spread_bank
 
         def fetch_cluster_norms(im):
@@ -373,21 +405,37 @@ def tile_salad_pa_k_kernel(tc, f_clu, h_score, W_s2, b_s2, burst_par, out):
         image0 = new_image(0)
         image1 = new_image(1)
 
-        for c in range(CHUNKS):
-            load_chunk(image0, c)
-        for c in range(CHUNKS):
-            empty_banks(
-                image0, c, transpose_chunk(image0, c), (nc.vector.tensor_copy, nc.vector.tensor_copy)
-            )
+        copies = (nc.scalar.copy, nc.vector.tensor_copy)
+
+        def turn_chunk_of_image0(c):
+            empty_banks(image0, c, transpose_chunk(image0, c), copies)
             if c >= 1:
                 quantise_turned(image0, c - 1)
-            if c % PAIR == PAIR - 1:
-                square_pair(image0, c // PAIR, range(PACK))
-        quantise_turned(image0, CHUNKS - 1)
-        soft_assignment(image0)
-        soft_assignment(image1)
-        pixel_norms(image0)
 
+        for c in range(EARLY):
+            load_chunk(image0, c)
+        load_hidden(image0)
+        load_hidden(image1)
+        for c in range(EARLY, CHUNKS):
+            load_chunk(image0, c)
+        gram = [sim_banks.tile([P, P], F32, name="gram%d" % m, tag="sim") for m in range(PACK)]
+        for c in range(CHUNKS):
+            add_to_gram(gram, image0["rows"][c], c == 0, c == CHUNKS - 1)
+            if c >= LAG:
+                turn_chunk_of_image0(c - LAG)
+            if c == EARLY:
+                soft_assignment(image0)
+                soft_assignment(image1)
+        inverse_norm0 = inverse_root(diagonals(gram), PACK)
+        for c in range(CHUNKS - LAG, CHUNKS):
+            turn_chunk_of_image0(c)
+        quantise_turned(image0, CHUNKS - 1)
+        spread_pixel_norms(image0, inverse_norm0, lambda spread, m: spread[:, m * P : (m + 1) * P])
+
+
+        image1["pixel_squares"] = small.tile(
+            [P, PACK, CHUNKS // PAIR], F32, name="pixel_squares", tag="pixel_squares"
+        )
 
         def load_next_chunk_of_image1():
             if len(image1["rows"]) < CHUNKS:
@@ -404,7 +452,7 @@ def tile_salad_pa_k_kernel(tc, f_clu, h_score, W_s2, b_s2, burst_par, out):
                 if not on_gpsimd(c):
                     scale_chunk(image0, c)
                     load_next_chunk_of_image1()
-                empty_banks(image1, c, two_banks, (nc.scalar.copy, nc.vector.tensor_copy))
+                empty_banks(image1, c, two_banks, copies)
                 if c + 1 < CHUNKS:
                     two_banks = transpose_chunk(image1, c + 1)
                 if c >= PAIR:
@@ -417,7 +465,11 @@ def tile_salad_pa_k_kernel(tc, f_clu, h_score, W_s2, b_s2, burst_par, out):
                 scale_chunk(image0, first + 2 * ROUND - 1)
                 load_next_chunk_of_image1()
         square_pair(image1, CHUNKS // PAIR - 1, range(PACK))
-        pixel_norms(image1)
+        spread_pixel_norms(
+            image1,
+            inverse_root(summed_squares(image1), PACK),
+            lambda spread, t: spread[:].rearrange("p (q t) -> p q t", t=PACK)[:, :, t],
+        )
         burst_weights(image0)
 
         scale_chunk(image1, ROUND - 1)

@@ -22,6 +22,7 @@ PACK = 4
 K_PASS = P * PACK
 CHUNKS = D_FEAT // K_PASS
 HALF = CHUNKS // 2
+QUARTER = CHUNKS // 4
 PAIR = 2
 EPS_NORM_SQUARED = 1e-24
 EPS_DENOM = 1e-6
@@ -72,11 +73,14 @@ def tile_salad_pa_k_kernel(tc, f_clu, h_score, W_s2, b_s2, burst_par, out):
             nc.sync.dma_start(out=rows[:], in_=dram_rows.rearrange("(p j) n -> p j n", j=PACK))
             return rows
 
-        def columns_by_slot(grouped):
-            return grouped[:].rearrange("p (t q) j -> p q j t", t=PACK)
-
         def pixels_by_slot(rows):
             return rows[:].rearrange("p j (q t) -> p q j t", t=PACK)
+
+        def columns_in_pixel_order(grouped):
+            return grouped[:].rearrange("p (q t) j -> p q j t", t=PACK)
+
+        def columns_by_slot(grouped):
+            return grouped[:].rearrange("p (t q) j -> p q j t", t=PACK)
 
         def quantise(grouped_columns, codes, scales):
             nc.vector.quantize_mx(
@@ -243,7 +247,7 @@ def tile_salad_pa_k_kernel(tc, f_clu, h_score, W_s2, b_s2, burst_par, out):
                     )
 
         def diagonals(gram):
-            on_diagonal = const.tile([P, PACK, P], F32)
+            on_diagonal = const.tile([P, PACK, P], F32, tag="masked")
             for m in range(PACK):
                 nc.vector.tensor_tensor(
                     out=on_diagonal[:, m, :], in0=gram[m][:], in1=ident[:], op=ALU.mult
@@ -278,7 +282,7 @@ def tile_salad_pa_k_kernel(tc, f_clu, h_score, W_s2, b_s2, burst_par, out):
                 grouped = pass_pool.tile([P, N_PIX, PACK], BF16, tag="grouped", align_bytes=64)
                 engine, norms = nc.vector, im["spread"]
             engine.tensor_tensor(
-                out=columns_by_slot(grouped),
+                out=columns_in_pixel_order(grouped),
                 in0=pixels_by_slot(im["rows"][c]),
                 in1=norms[:]
                 .rearrange("p (q t) -> p q t", t=PACK)
@@ -291,32 +295,48 @@ def tile_salad_pa_k_kernel(tc, f_clu, h_score, W_s2, b_s2, burst_par, out):
         def similarity_pass(im, c):
             if c == 0:
                 im["sim"] = [
-                    sim_banks.tile([P, N_PIX], F32, name="sim%d" % t, tag="sim") for t in range(PACK)
+                    sim_banks.tile([P, N_PIX], F32, name="sim%d" % m, tag="sim") for m in range(PACK)
                 ]
             fn_codes, fn_scales = quantise_pass(im["scaled"][c])
-            for t in range(PACK):
+            for m in range(PACK):
                 nc.tensor.matmul_mx(
-                    out=im["sim"][t][:],
-                    lhsT=fn_codes[:, t * P : (t + 1) * P].bitcast(FP8X4),
-                    lhsT_scale=fn_scales[:, t * P : (t + 1) * P],
+                    out=im["sim"][m][:],
+                    lhsT=fn_codes[:, m * P : (m + 1) * P].bitcast(FP8X4),
+                    lhsT_scale=fn_scales[:, m * P : (m + 1) * P],
                     rhs=fn_codes[:].bitcast(FP8X4),
                     rhs_scale=fn_scales[:],
                     start=(c == 0),
                     stop=(c == CHUNKS - 1),
                 )
 
-        def burst_weights(im):
-            w = small.tile([P, PACK], F32, tag="w")
-            for t in range(PACK):
+        def burst_sums(im):
+            w_by_block = small.tile([P, PACK], F32, tag="w_by_block")
+            for m in range(PACK):
                 unread = unread_pool.tile([P, N_PIX], BF16, tag="bank_wide")
                 nc.scalar.activation(
                     out=unread[:],
-                    in_=im["sim"][t][:],
+                    in_=im["sim"][m][:],
                     func=ACT.Sigmoid,
                     scale=par[:, 0:1],
                     bias=par[:, 1:2],
-                    accum_out=w[:, t : t + 1],
+                    accum_out=w_by_block[:, m : m + 1],
                 )
+            im["w_by_block"] = w_by_block
+
+        def burst_power(im):
+            everywhere = banks.tile([P, N_PIX], F32, tag="bank")
+            spread_over_partitions(
+                [everywhere[:, m * P : (m + 1) * P] for m in range(PACK)], im["w_by_block"]
+            )
+            own = const.tile([P, PACK, P], F32, tag="masked")
+            nc.vector.tensor_tensor(
+                out=own[:].rearrange("p t q -> p q t"),
+                in0=everywhere[:].rearrange("p (q t) -> p q t", t=PACK),
+                in1=ident[:].unsqueeze(2).to_broadcast([P, P, PACK]),
+                op=ALU.mult,
+            )
+            w = small.tile([P, PACK], F32, tag="w")
+            nc.vector.tensor_reduce(out=w[:], in_=own[:], axis=AXIS.X, op=ALU.add)
             w_power = small.tile([P, PACK], F32, tag="w_power")
             nc.gpsimd.tensor_tensor(out=w_power[:], in0=w[:], in1=exponent[:], op=ALU.pow)
             im["w_power"] = w_power
@@ -470,7 +490,7 @@ def tile_salad_pa_k_kernel(tc, f_clu, h_score, W_s2, b_s2, burst_par, out):
             inverse_root(summed_squares(image1), PACK),
             lambda spread, t: spread[:].rearrange("p (q t) -> p q t", t=PACK)[:, :, t],
         )
-        burst_weights(image0)
+        burst_sums(image0)
 
         scale_chunk(image1, ROUND - 1)
         for first in range(0, CHUNKS, ROUND):
@@ -479,21 +499,26 @@ def tile_salad_pa_k_kernel(tc, f_clu, h_score, W_s2, b_s2, burst_par, out):
                 if not on_gpsimd(c):
                     scale_chunk(image1, c)
             if first == 0:
+                burst_power(image0)
+            if first == ROUND:
                 weighted_assignment(image0)
             for c in members:
                 similarity_pass(image1, c)
             if first + 2 * ROUND - 1 < CHUNKS:
                 scale_chunk(image1, first + 2 * ROUND - 1)
             for c in members:
-                if c < HALF:
-                    square_aggregate(image0, 2 * c)
-                    square_aggregate(image0, 2 * c + 1)
-            if HALF - 1 + ROUND in members:
+                if ROUND <= c < ROUND + HALF:
+                    square_aggregate(image0, 2 * (c - ROUND))
+                    square_aggregate(image0, 2 * (c - ROUND) + 1)
+            if HALF - 1 + 2 * ROUND in members:
                 cluster_norms(image0)
 
-        burst_weights(image1)
+        burst_sums(image1)
         fetch_cluster_norms(image0)
-        for c in range(HALF):
+        for c in range(QUARTER):
+            output_chunk(image0, c)
+        burst_power(image1)
+        for c in range(QUARTER, HALF):
             output_chunk(image0, c)
         weighted_assignment(image1)
         for c in range(CHUNKS):

@@ -22,14 +22,15 @@ PACK = 4
 K_PASS = P * PACK
 CHUNKS = D_FEAT // K_PASS
 HALF = CHUNKS // 2
-QUARTER = CHUNKS // 4
 PAIR = 2
 EPS_NORM_SQUARED = 1e-24
 EPS_DENOM = 1e-6
-ROW_TILES = 18
+ROW_TILES = 21
+SHIFT = 3
 EARLY = 4
 LAG = 2
 ROUND = 3
+ROUND_ALONE = 4
 
 FLOPS = 2 * IMAGES * (K_CLU * F_HID * N_PIX + N_PIX * D_FEAT * N_PIX + D_FEAT * N_PIX * K_CLU)
 
@@ -73,14 +74,11 @@ def tile_salad_pa_k_kernel(tc, f_clu, h_score, W_s2, b_s2, burst_par, out):
             nc.sync.dma_start(out=rows[:], in_=dram_rows.rearrange("(p j) n -> p j n", j=PACK))
             return rows
 
-        def pixels_by_slot(rows):
-            return rows[:].rearrange("p j (q t) -> p q j t", t=PACK)
-
-        def columns_in_pixel_order(grouped):
-            return grouped[:].rearrange("p (q t) j -> p q j t", t=PACK)
-
         def columns_by_slot(grouped):
             return grouped[:].rearrange("p (t q) j -> p q j t", t=PACK)
+
+        def pixels_by_slot(rows):
+            return rows[:].rearrange("p j (q t) -> p q j t", t=PACK)
 
         def quantise(grouped_columns, codes, scales):
             nc.vector.quantize_mx(
@@ -106,7 +104,7 @@ def tile_salad_pa_k_kernel(tc, f_clu, h_score, W_s2, b_s2, burst_par, out):
 
         def spread_over_partitions(bank_views, per_partition):
             width = len(bank_views)
-            repeated = const.tile([P, width, P], F32, tag="repeated%d" % width)
+            repeated = const.tile([P, width, P], F32, tag="work%d" % width)
             nc.vector.tensor_copy(
                 out=repeated[:], in_=per_partition[:].unsqueeze(2).to_broadcast([P, width, P])
             )
@@ -247,7 +245,7 @@ def tile_salad_pa_k_kernel(tc, f_clu, h_score, W_s2, b_s2, burst_par, out):
                     )
 
         def diagonals(gram):
-            on_diagonal = const.tile([P, PACK, P], F32, tag="masked")
+            on_diagonal = const.tile([P, PACK, P], F32, tag="work%d" % PACK)
             for m in range(PACK):
                 nc.vector.tensor_tensor(
                     out=on_diagonal[:, m, :], in0=gram[m][:], in1=ident[:], op=ALU.mult
@@ -271,18 +269,15 @@ def tile_salad_pa_k_kernel(tc, f_clu, h_score, W_s2, b_s2, burst_par, out):
             im["spread"] = spread
             im["spread_copy"] = spread_copy
 
-        def on_gpsimd(c):
-            return c % ROUND == ROUND - 1
-
-        def scale_chunk(im, c):
-            if on_gpsimd(c):
+        def scale_chunk(im, c, on_gpsimd):
+            if on_gpsimd:
                 grouped = gpsimd_pool.tile([P, N_PIX, PACK], BF16, tag="grouped", align_bytes=64)
                 engine, norms = nc.gpsimd, im["spread_copy"]
             else:
                 grouped = pass_pool.tile([P, N_PIX, PACK], BF16, tag="grouped", align_bytes=64)
                 engine, norms = nc.vector, im["spread"]
             engine.tensor_tensor(
-                out=columns_in_pixel_order(grouped),
+                out=columns_by_slot(grouped),
                 in0=pixels_by_slot(im["rows"][c]),
                 in1=norms[:]
                 .rearrange("p (q t) -> p q t", t=PACK)
@@ -295,48 +290,32 @@ def tile_salad_pa_k_kernel(tc, f_clu, h_score, W_s2, b_s2, burst_par, out):
         def similarity_pass(im, c):
             if c == 0:
                 im["sim"] = [
-                    sim_banks.tile([P, N_PIX], F32, name="sim%d" % m, tag="sim") for m in range(PACK)
+                    sim_banks.tile([P, N_PIX], F32, name="sim%d" % t, tag="sim") for t in range(PACK)
                 ]
             fn_codes, fn_scales = quantise_pass(im["scaled"][c])
-            for m in range(PACK):
+            for t in range(PACK):
                 nc.tensor.matmul_mx(
-                    out=im["sim"][m][:],
-                    lhsT=fn_codes[:, m * P : (m + 1) * P].bitcast(FP8X4),
-                    lhsT_scale=fn_scales[:, m * P : (m + 1) * P],
+                    out=im["sim"][t][:],
+                    lhsT=fn_codes[:, t * P : (t + 1) * P].bitcast(FP8X4),
+                    lhsT_scale=fn_scales[:, t * P : (t + 1) * P],
                     rhs=fn_codes[:].bitcast(FP8X4),
                     rhs_scale=fn_scales[:],
                     start=(c == 0),
                     stop=(c == CHUNKS - 1),
                 )
 
-        def burst_sums(im):
-            w_by_block = small.tile([P, PACK], F32, tag="w_by_block")
-            for m in range(PACK):
+        def burst_weights(im):
+            w = small.tile([P, PACK], F32, tag="w")
+            for t in range(PACK):
                 unread = unread_pool.tile([P, N_PIX], BF16, tag="bank_wide")
                 nc.scalar.activation(
                     out=unread[:],
-                    in_=im["sim"][m][:],
+                    in_=im["sim"][t][:],
                     func=ACT.Sigmoid,
                     scale=par[:, 0:1],
                     bias=par[:, 1:2],
-                    accum_out=w_by_block[:, m : m + 1],
+                    accum_out=w[:, t : t + 1],
                 )
-            im["w_by_block"] = w_by_block
-
-        def burst_power(im):
-            everywhere = banks.tile([P, N_PIX], F32, tag="bank")
-            spread_over_partitions(
-                [everywhere[:, m * P : (m + 1) * P] for m in range(PACK)], im["w_by_block"]
-            )
-            own = const.tile([P, PACK, P], F32, tag="masked")
-            nc.vector.tensor_tensor(
-                out=own[:].rearrange("p t q -> p q t"),
-                in0=everywhere[:].rearrange("p (q t) -> p q t", t=PACK),
-                in1=ident[:].unsqueeze(2).to_broadcast([P, P, PACK]),
-                op=ALU.mult,
-            )
-            w = small.tile([P, PACK], F32, tag="w")
-            nc.vector.tensor_reduce(out=w[:], in_=own[:], axis=AXIS.X, op=ALU.add)
             w_power = small.tile([P, PACK], F32, tag="w_power")
             nc.gpsimd.tensor_tensor(out=w_power[:], in0=w[:], in1=exponent[:], op=ALU.pow)
             im["w_power"] = w_power
@@ -461,64 +440,68 @@ def tile_salad_pa_k_kernel(tc, f_clu, h_score, W_s2, b_s2, burst_par, out):
             if len(image1["rows"]) < CHUNKS:
                 load_chunk(image1, len(image1["rows"]))
 
-        load_next_chunk_of_image1()
-        load_next_chunk_of_image1()
-        scale_chunk(image0, ROUND - 1)
-        load_next_chunk_of_image1()
-        two_banks = transpose_chunk(image1, 0)
-        for first in range(0, CHUNKS, ROUND):
-            members = range(first, min(first + ROUND, CHUNKS))
-            for c in members:
-                if not on_gpsimd(c):
-                    scale_chunk(image0, c)
-                    load_next_chunk_of_image1()
-                empty_banks(image1, c, two_banks, copies)
-                if c + 1 < CHUNKS:
-                    two_banks = transpose_chunk(image1, c + 1)
-                if c >= PAIR:
-                    square_pair(image1, c // PAIR - 1, (2 * (c % PAIR), 2 * (c % PAIR) + 1))
-            for c in members:
-                quantise_turned(image1, c)
-            for c in members:
+        def scale_chunk_of_image0(c, on_gpsimd):
+            scale_chunk(image0, c, on_gpsimd)
+            load_next_chunk_of_image1()
+
+        def turn_step_of_image1(x):
+            if x < CHUNKS:
+                empty_banks(image1, x, image1["banks"], copies)
+            if x + 1 < CHUNKS:
+                image1["banks"] = transpose_chunk(image1, x + 1)
+            if PAIR <= x < CHUNKS + PAIR:
+                square_pair(image1, x // PAIR - 1, (2 * (x % PAIR), 2 * (x % PAIR) + 1))
+
+        for spare in range(ROW_TILES - CHUNKS):
+            load_next_chunk_of_image1()
+        scale_chunk_of_image0(ROUND - 1, True)
+        image1["banks"] = transpose_chunk(image1, 0)
+        for first in range(0, CHUNKS - 1, ROUND):
+            for c in range(first, first + ROUND):
+                if c < first + ROUND - 1:
+                    scale_chunk_of_image0(c, False)
+                if first == 0:
+                    turn_step_of_image1(2 * c)
+                    turn_step_of_image1(2 * c + 1)
+                else:
+                    turn_step_of_image1(c + SHIFT)
+            for x in range(0 if first == 0 else first + SHIFT, min(first + ROUND + SHIFT, CHUNKS)):
+                quantise_turned(image1, x)
+            for c in range(first, first + ROUND):
                 similarity_pass(image0, c)
             if first + 2 * ROUND - 1 < CHUNKS:
-                scale_chunk(image0, first + 2 * ROUND - 1)
-                load_next_chunk_of_image1()
-        square_pair(image1, CHUNKS // PAIR - 1, range(PACK))
+                scale_chunk_of_image0(first + 2 * ROUND - 1, True)
+        scale_chunk_of_image0(CHUNKS - 1, False)
+        inverse_norm1 = inverse_root(summed_squares(image1), PACK)
+        similarity_pass(image0, CHUNKS - 1)
         spread_pixel_norms(
             image1,
-            inverse_root(summed_squares(image1), PACK),
+            inverse_norm1,
             lambda spread, t: spread[:].rearrange("p (q t) -> p q t", t=PACK)[:, :, t],
         )
-        burst_sums(image0)
 
-        scale_chunk(image1, ROUND - 1)
-        for first in range(0, CHUNKS, ROUND):
-            members = range(first, min(first + ROUND, CHUNKS))
-            for c in members:
-                if not on_gpsimd(c):
-                    scale_chunk(image1, c)
+        scale_chunk(image1, ROUND_ALONE - 1, True)
+        burst_weights(image0)
+        for first in range(0, CHUNKS, ROUND_ALONE):
+            members = range(first, first + ROUND_ALONE)
+            for c in range(first, first + ROUND_ALONE - 1):
+                scale_chunk(image1, c, False)
             if first == 0:
-                burst_power(image0)
-            if first == ROUND:
                 weighted_assignment(image0)
             for c in members:
                 similarity_pass(image1, c)
-            if first + 2 * ROUND - 1 < CHUNKS:
-                scale_chunk(image1, first + 2 * ROUND - 1)
+            if first + 2 * ROUND_ALONE - 1 < CHUNKS:
+                scale_chunk(image1, first + 2 * ROUND_ALONE - 1, True)
             for c in members:
-                if ROUND <= c < ROUND + HALF:
-                    square_aggregate(image0, 2 * (c - ROUND))
-                    square_aggregate(image0, 2 * (c - ROUND) + 1)
-            if HALF - 1 + 2 * ROUND in members:
+                if c < HALF:
+                    square_aggregate(image0, 2 * c)
+                    square_aggregate(image0, 2 * c + 1)
+            if HALF - 1 + ROUND_ALONE in members:
                 cluster_norms(image0)
 
-        burst_sums(image1)
+        burst_weights(image1)
         fetch_cluster_norms(image0)
-        for c in range(QUARTER):
-            output_chunk(image0, c)
-        burst_power(image1)
-        for c in range(QUARTER, HALF):
+        for c in range(HALF):
             output_chunk(image0, c)
         weighted_assignment(image1)
         for c in range(CHUNKS):

@@ -49,6 +49,7 @@ def tile_salad_pa_k_kernel(tc, f_clu, h_score, W_s2, b_s2, burst_par, out):
         sim_banks = ctx.enter_context(tc.psum_pool(name="sim_banks", bufs=PACK))
         norm_bank = ctx.enter_context(tc.psum_pool(name="norm_bank", bufs=1))
         banks = ctx.enter_context(tc.psum_pool(name="banks", bufs=3))
+        ctx.enter_context(tc.manual_schedule())
 
         ident = const.tile([P, P], F32)
         make_identity(nc, ident[:])

@@ -22,13 +22,12 @@ PACK = 4
 K_PASS = P * PACK
 CHUNKS = D_FEAT // K_PASS
 HALF = CHUNKS // 2
-PAIR = 2
 EPS_NORM_SQUARED = 1e-24
 EPS_DENOM = 1e-6
 ROW_TILES = 21
-SHIFT = 3
-EARLY = 4
-LAG = 2
+EARLY = 7
+SQUARED0 = 6
+GRAM1 = 3
 ROUND = 3
 ROUND_ALONE = 4
 
@@ -40,35 +39,35 @@ def tile_salad_pa_k_kernel(tc, f_clu, h_score, W_s2, b_s2, burst_par, out):
     with ExitStack() as ctx:
         const = ctx.enter_context(tc.tile_pool(name="const", bufs=1))
         rows_pool = ctx.enter_context(tc.tile_pool(name="rows", bufs=ROW_TILES))
-        turned_pool = ctx.enter_context(tc.tile_pool(name="turned", bufs=3))
+        turned_pool = ctx.enter_context(tc.tile_pool(name="turned", bufs=6))
         image_pool = ctx.enter_context(tc.tile_pool(name="image", bufs=IMAGES))
         pass_pool = ctx.enter_context(tc.tile_pool(name="pass", bufs=3))
+        codes_pool = ctx.enter_context(tc.tile_pool(name="codes", bufs=4))
         gpsimd_pool = ctx.enter_context(tc.tile_pool(name="gpsimd", bufs=1))
         unread_pool = ctx.enter_context(tc.tile_pool(name="unread", bufs=2))
         small = ctx.enter_context(tc.tile_pool(name="small", bufs=2))
         sim_banks = ctx.enter_context(tc.psum_pool(name="sim_banks", bufs=PACK))
         norm_bank = ctx.enter_context(tc.psum_pool(name="norm_bank", bufs=1))
         banks = ctx.enter_context(tc.psum_pool(name="banks", bufs=3))
+
         ctx.enter_context(tc.manual_schedule())
 
         ident = const.tile([P, P], F32)
         make_identity(nc, ident[:])
-        minus_half = const.tile([P, PACK], F32)
-        nc.vector.memset(minus_half[:], -0.5)
         first_exp = const.tile([P, 1], F32)
         nc.vector.memset(first_exp[:], 0.0)
         nc.scalar.activation(out=first_exp[:], in_=first_exp[:], func=ACT.Exp)
 
-        par_bf = const.tile([P, 3], BF16)
-        nc.scalar.dma_start(out=par_bf[:], in_=burst_par.partition_broadcast(P))
-        par = const.tile([P, 3], F32)
-        nc.vector.tensor_copy(out=par[:], in_=par_bf[:])
-        exponent = const.tile([P, PACK], F32)
-        nc.vector.tensor_copy(out=exponent[:], in_=par_bf[:, 2:3].to_broadcast([P, PACK]))
-        bias = const.tile([P, K_CLU], BF16)
-        nc.scalar.dma_start(out=bias[:], in_=b_s2.partition_broadcast(P))
         w_rows = const.tile([K_CLU, F_HID], BF16)
         nc.scalar.dma_start(out=w_rows[:], in_=W_s2)
+        row = const.tile([P, K_CLU + PACK], BF16)
+        nc.vector.memset(row[:], 0.0)
+        nc.scalar.dma_start(out=row[0:1, 0:K_CLU], in_=b_s2.unsqueeze(0))
+        nc.scalar.dma_start(out=row[0:1, K_CLU : K_CLU + 3], in_=burst_par.unsqueeze(0))
+        ones = const.tile([P, P], BF16)
+        nc.vector.memset(ones[:], 1.0)
+        minus_half = const.tile([P, PACK], F32)
+        nc.vector.memset(minus_half[:], -0.5)
 
         def load_rows(dram_rows):
             rows = rows_pool.tile([P, PACK, N_PIX], BF16, tag="rows")
@@ -89,8 +88,8 @@ def tile_salad_pa_k_kernel(tc, f_clu, h_score, W_s2, b_s2, burst_par, out):
             )
 
         def quantise_pass(grouped):
-            codes = pass_pool.tile([P, N_PIX], U32, tag="codes", align_bytes=64)
-            scales = pass_pool.tile([P, N_PIX], U8, tag="scales", align_bytes=64)
+            codes = codes_pool.tile([P, N_PIX], U32, tag="codes", align_bytes=64)
+            scales = codes_pool.tile([P, N_PIX], U8, tag="scales", align_bytes=64)
             quantise(grouped[:], codes[:], scales[:])
             return codes, scales
 
@@ -104,31 +103,40 @@ def tile_salad_pa_k_kernel(tc, f_clu, h_score, W_s2, b_s2, burst_par, out):
             return inverse
 
         def spread_over_partitions(bank_views, per_partition):
-            width = len(bank_views)
-            repeated = const.tile([P, width, P], F32, tag="work%d" % width)
-            nc.vector.tensor_copy(
-                out=repeated[:], in_=per_partition[:].unsqueeze(2).to_broadcast([P, width, P])
-            )
-            for k in range(width):
-                nc.tensor.transpose(bank_views[k], repeated[:, k, :], ident[:])
+            for k, view in enumerate(bank_views):
+                nc.tensor.transpose(view, per_partition[:, k : k + 1].to_broadcast([P, P]), ident[:])
 
-        w_words = w_rows[:].bitcast(F32).rearrange("k (q u) -> k u q", u=2)
-        w_turned = banks.tile([P, 2, K_CLU], F32, tag="bank")
-        for u in range(2):
-            nc.tensor.transpose(w_turned[:, u, :], w_words[:, u, :], ident[:])
-        w_grouped = const.tile([P, K_CLU, PACK], BF16, align_bytes=64)
-        nc.vector.tensor_copy(
-            out=w_grouped[:].bitcast(F32), in_=w_turned[:].rearrange("q u k -> q k u")
-        )
-        w_codes = const.tile([P, K_CLU], U32, align_bytes=64)
-        w_scales = const.tile([P, K_CLU], U8, align_bytes=64)
-        quantise(w_grouped[:], w_codes[:], w_scales[:])
+        def fetch_parameters():
+            spread_row = banks.tile([P, K_CLU + PACK], F32, name="spread_row", tag="bank")
+            nc.tensor.matmul(out=spread_row[:], lhsT=ones[:], rhs=row[:], start=True, stop=True)
+            held = const.tile([P, K_CLU + PACK], F32, name="held")
+            nc.vector.tensor_copy(out=held[:], in_=spread_row[:])
+            exponent = const.tile([P, PACK], F32, name="exponent")
+            nc.vector.tensor_copy(
+                out=exponent[:], in_=held[:, K_CLU + 2 : K_CLU + 3].to_broadcast([P, PACK])
+            )
+            return held, exponent
+
+        def quantise_w():
+            w_words = w_rows[:].bitcast(F32).rearrange("k (q u) -> k u q", u=2)
+            w_turned = banks.tile([P, 2, K_CLU], F32, name="w_turned", tag="bank")
+            for u in range(2):
+                nc.tensor.transpose(w_turned[:, u, :], w_words[:, u, :], ident[:])
+            w_grouped = const.tile([P, K_CLU, PACK], BF16, name="w_grouped", align_bytes=64)
+            nc.vector.tensor_copy(
+                out=w_grouped[:].bitcast(F32), in_=w_turned[:].rearrange("q u k -> q k u")
+            )
+            w_codes = const.tile([P, K_CLU], U32, name="w_codes", align_bytes=64)
+            w_scales = const.tile([P, K_CLU], U8, name="w_scales", align_bytes=64)
+            quantise(w_grouped[:], w_codes[:], w_scales[:])
+            return w_codes, w_scales
 
         def new_image(i):
             return {
                 "index": i,
                 "rows": [],
-                "turned": [],
+                "banks": {},
+                "turned": {},
                 "scaled": {},
                 "fT_codes": image_pool.tile(
                     [P, D_FEAT], U32, name="fT_codes", tag="fT_codes", align_bytes=64
@@ -144,61 +152,55 @@ def tile_salad_pa_k_kernel(tc, f_clu, h_score, W_s2, b_s2, burst_par, out):
         def load_chunk(im, c):
             im["rows"].append(load_rows(f_clu[im["index"], c * K_PASS : (c + 1) * K_PASS, :]))
 
-        def transpose_chunk(im, c):
+        def transpose_chunk(im, c, pools=None):
             words = im["rows"][c][:].bitcast(F32).rearrange("p j (q u) -> p j u q", u=2)
-            two_banks = []
+            im["banks"][c] = []
             for half in range(2):
-                bank = banks.tile([P, 2, 2, P], F32, name="turned_bank", tag="bank")
+                pool, tag = (banks, "bank") if pools is None else pools[half]
+                bank = pool.tile([P, 2, 2, P], F32, name="turned_bank", tag=tag)
                 for jj in range(2):
                     for u in range(2):
                         nc.tensor.transpose(bank[:, jj, u, :], words[:, 2 * half + jj, u, :], ident[:])
-                two_banks.append(bank)
-            return two_banks
+                im["banks"][c].append(bank)
 
-        def empty_banks(im, c, two_banks, copies):
-            if c % PAIR == 0:
-                im["turned"].append(
-                    turned_pool.tile(
-                        [P, PAIR * K_PASS, PACK], BF16, name="turned", tag="turned", align_bytes=64
-                    )
-                )
-            turned_words = im["turned"][c // PAIR][:].bitcast(F32)
+        def empty_banks(im, c, copies):
+            turned = turned_pool.tile([P, K_PASS, PACK], BF16, name="turned", tag="turned", align_bytes=64)
+            turned_words = turned[:].bitcast(F32)
             for half in range(2):
-                first = (c % PAIR) * K_PASS + half * 2 * P
+                first = half * 2 * P
                 copies[half](
                     out=turned_words[:, first : first + 2 * P, :].rearrange(
                         "q (jj p) u -> q jj p u", jj=2
                     ),
-                    in_=two_banks[half][:].rearrange("q jj u p -> q jj p u"),
+                    in_=im["banks"][c][half][:].rearrange("q jj u p -> q jj p u"),
                 )
+            im["turned"][c] = turned
 
         def quantise_turned(im, c):
             columns = slice(c * K_PASS, (c + 1) * K_PASS)
-            first = (c % PAIR) * K_PASS
-            quantise(
-                im["turned"][c // PAIR][:, first : first + K_PASS, :],
-                im["fT_codes"][:, columns],
-                im["fT_scales"][:, columns],
-            )
+            quantise(im["turned"][c][:], im["fT_codes"][:, columns], im["fT_scales"][:, columns])
 
-        def square_pair(im, pair, slots):
-            for t in slots:
-                unread = unread_pool.tile([P, PAIR * K_PASS], BF16, tag="squares")
+        def square_chunk(im, c):
+            for t in range(PACK):
+                unread = unread_pool.tile([P, K_PASS], BF16, tag="bank_wide")
                 nc.scalar.activation(
                     out=unread[:],
-                    in_=im["turned"][pair][:, :, t],
+                    in_=im["turned"][c][:, :, t],
                     func=ACT.Square,
-                    accum_out=im["pixel_squares"][:, t, pair : pair + 1],
+                    accum_out=im["pixel_squares"][:, t, im["measured"] : im["measured"] + 1],
                 )
+            im["measured"] += 1
 
         def load_hidden(im):
             im["h_rows"] = load_rows(h_score[im["index"]])
 
-        def soft_assignment(im):
-            h_rows = im["h_rows"]
+        def quantise_hidden(im):
             h_grouped = pass_pool.tile([P, N_PIX, PACK], BF16, tag="grouped", align_bytes=64)
-            nc.vector.tensor_copy(out=columns_by_slot(h_grouped), in_=pixels_by_slot(h_rows))
-            h_codes, h_scales = quantise_pass(h_grouped)
+            nc.vector.tensor_copy(out=columns_by_slot(h_grouped), in_=pixels_by_slot(im["h_rows"]))
+            im["h"] = quantise_pass(h_grouped)
+
+        def soft_assignment(im):
+            h_codes, h_scales = im["h"]
             product = banks.tile([P, PACK, K_CLU], F32, tag="bank")
             for t in range(PACK):
                 nc.tensor.matmul_mx(
@@ -214,7 +216,7 @@ def tile_salad_pa_k_kernel(tc, f_clu, h_score, W_s2, b_s2, burst_par, out):
             nc.vector.tensor_tensor(
                 out=expo[:],
                 in0=product[:],
-                in1=bias[:].unsqueeze(1).to_broadcast([P, PACK, K_CLU]),
+                in1=held[:, 0:K_CLU].unsqueeze(1).to_broadcast([P, PACK, K_CLU]),
                 op=ALU.add,
             )
             top = small.tile([P, PACK], F32, tag="top")
@@ -245,29 +247,48 @@ def tile_salad_pa_k_kernel(tc, f_clu, h_score, W_s2, b_s2, burst_par, out):
                         stop=(last and j == PACK - 1),
                     )
 
-        def diagonals(gram):
-            on_diagonal = const.tile([P, PACK, P], F32, tag="work%d" % PACK)
+        def gram_diagonals(gram, extra):
+            width = P + (0 if extra is None else 1)
+            on_diagonal = const.tile([P, PACK, P + PACK], F32, tag="on_diagonal")
             for m in range(PACK):
                 nc.vector.tensor_tensor(
-                    out=on_diagonal[:, m, :], in0=gram[m][:], in1=ident[:], op=ALU.mult
+                    out=on_diagonal[:, m, 0:P], in0=gram[m][:], in1=ident[:], op=ALU.mult
                 )
-            squared_norm = small.tile([P, PACK], F32, tag="squared_norm")
-            nc.vector.tensor_reduce(out=squared_norm[:], in_=on_diagonal[:], axis=AXIS.X, op=ALU.add)
-            return squared_norm
+            if extra is not None:
+                nc.vector.tensor_copy(out=on_diagonal[:, :, P], in_=extra[:])
+            squares = small.tile([P, PACK], F32, tag="gram_squares")
+            nc.vector.tensor_reduce(out=squares[:], in_=on_diagonal[:, :, 0:width], axis=AXIS.X, op=ALU.add)
+            return squares
 
-        def summed_squares(im):
-            squared_norm = small.tile([P, PACK], F32, tag="squared_norm")
-            nc.vector.tensor_reduce(
-                out=squared_norm[:], in_=im["pixel_squares"][:], axis=AXIS.X, op=ALU.add
+        def by_block(bank):
+            return bank[:].rearrange("p (m i) -> p m i", m=PACK)
+
+        def by_slot(bank):
+            return bank[:].rearrange("p (q t) -> p t q", t=PACK)
+
+        def reorder(per_pixel, source, target):
+            spread = banks.tile([P, N_PIX], F32, name="reorder_bank", tag="bank")
+            spread_over_partitions([source(spread)[:, k, :] for k in range(PACK)], per_pixel)
+            kept = const.tile([P, PACK, P + PACK], F32, tag="on_diagonal")
+            nc.vector.tensor_tensor(
+                out=kept[:, :, 0:P],
+                in0=target(spread),
+                in1=ident[:].unsqueeze(1).to_broadcast([P, PACK, P]),
+                op=ALU.mult,
             )
-            return squared_norm
+            return kept[:, :, 0:P]
 
-        def spread_pixel_norms(im, inverse_norm, pixels_of_column):
+        def sum_last(values, out):
+            nc.vector.tensor_reduce(out=out, in_=values, axis=AXIS.X, op=ALU.add)
+
+        def spread_pixel_norms(im, inverse_norm, order):
             spread = norm_bank.tile([P, N_PIX], F32, tag="spread")
-            spread_over_partitions([pixels_of_column(spread, k) for k in range(PACK)], inverse_norm)
-            spread_copy = const.tile([P, N_PIX], F32, tag="spread_copy")
-            nc.vector.tensor_copy(out=spread_copy[:], in_=spread[:])
+            spread_over_partitions([order(spread)[:, k, :] for k in range(PACK)], inverse_norm)
             im["spread"] = spread
+
+        def copy_pixel_norms(im):
+            spread_copy = const.tile([P, N_PIX], F32, tag="spread_copy")
+            nc.vector.tensor_copy(out=spread_copy[:], in_=im["spread"][:])
             im["spread_copy"] = spread_copy
 
         def scale_chunk(im, c, on_gpsimd):
@@ -313,8 +334,8 @@ def tile_salad_pa_k_kernel(tc, f_clu, h_score, W_s2, b_s2, burst_par, out):
                     out=unread[:],
                     in_=im["sim"][t][:],
                     func=ACT.Sigmoid,
-                    scale=par[:, 0:1],
-                    bias=par[:, 1:2],
+                    scale=held[:, K_CLU : K_CLU + 1],
+                    bias=held[:, K_CLU + 1 : K_CLU + 2],
                     accum_out=w[:, t : t + 1],
                 )
             w_power = small.tile([P, PACK], F32, tag="w_power")
@@ -404,13 +425,11 @@ def tile_salad_pa_k_kernel(tc, f_clu, h_score, W_s2, b_s2, burst_par, out):
 
         image0 = new_image(0)
         image1 = new_image(1)
-
-        copies = (nc.scalar.copy, nc.vector.tensor_copy)
-
-        def turn_chunk_of_image0(c):
-            empty_banks(image0, c, transpose_chunk(image0, c), copies)
-            if c >= 1:
-                quantise_turned(image0, c - 1)
+        for im, slots in ((image0, SQUARED0), (image1, CHUNKS - GRAM1 + 1)):
+            im["measured"] = 0
+            im["pixel_squares"] = small.tile(
+                [P, PACK, slots], F32, name="pixel_squares", tag="pixel_squares%d" % im["index"]
+            )
 
         for c in range(EARLY):
             load_chunk(image0, c)
@@ -418,87 +437,146 @@ def tile_salad_pa_k_kernel(tc, f_clu, h_score, W_s2, b_s2, burst_par, out):
         load_hidden(image1)
         for c in range(EARLY, CHUNKS):
             load_chunk(image0, c)
-        gram = [sim_banks.tile([P, P], F32, name="gram%d" % m, tag="sim") for m in range(PACK)]
+        for c in range(ROW_TILES - CHUNKS - IMAGES):
+            load_chunk(image1, c)
+
+        on_scalar = (nc.scalar.copy, nc.scalar.copy)
+        on_vector = (nc.vector.tensor_copy, nc.vector.tensor_copy)
+        on_both = (nc.scalar.copy, nc.vector.tensor_copy)
+
         for c in range(CHUNKS):
-            add_to_gram(gram, image0["rows"][c], c == 0, c == CHUNKS - 1)
-            if c >= LAG:
-                turn_chunk_of_image0(c - LAG)
-            if c == EARLY:
+            if c == SQUARED0:
+                gram = [sim_banks.tile([P, P], F32, name="gram%d" % m, tag="sim") for m in range(PACK)]
+            if c < SQUARED0:
+                transpose_chunk(image0, c, ((sim_banks, "sim"), (sim_banks, "sim")) if c % 2 == 0 else None)
+            else:
+                add_to_gram(gram, image0["rows"][c], c == SQUARED0, c == CHUNKS - 1)
+            if 1 <= c <= SQUARED0:
+                empty_banks(image0, c - 1, on_vector)
+                square_chunk(image0, c - 1)
+            if 2 <= c <= SQUARED0 + 1:
+                quantise_turned(image0, c - 2)
+            if c == SQUARED0 + 1:
+                held, exponent = fetch_parameters()
+                w_codes, w_scales = quantise_w()
+                quantise_hidden(image0)
+                quantise_hidden(image1)
+                for c1 in range(IMAGES):
+                    load_chunk(image1, len(image1["rows"]))
+            if c == SQUARED0 + 5:
                 soft_assignment(image0)
                 soft_assignment(image1)
-        inverse_norm0 = inverse_root(diagonals(gram), PACK)
-        for c in range(CHUNKS - LAG, CHUNKS):
-            turn_chunk_of_image0(c)
-        quantise_turned(image0, CHUNKS - 1)
-        spread_pixel_norms(image0, inverse_norm0, lambda spread, m: spread[:, m * P : (m + 1) * P])
+        rest0 = [(image0, c) for c in range(SQUARED0, CHUNKS)]
+        rest1 = [(image1, c) for c in range(GRAM1, CHUNKS)]
+        pattern = [0, 1, 0, 1, 0] + 4 * [1, 0, 1, 1] + [0] * 16
+        turns = []
+        for which in pattern:
+            source = rest1 if which else rest0
+            if source:
+                turns.append(source[0])
+                source.remove(source[0])
+        turns += rest0 + rest1 + [(image1, c) for c in range(GRAM1)]
+        last_measured = turns.index((image1, CHUNKS - 1))
+        turned_so_far = []
+        waiting = []
+        to_square = []
 
+        def square_waiting():
+            for im, c in to_square:
+                square_chunk(im, c)
+            to_square.clear()
 
-        image1["pixel_squares"] = small.tile(
-            [P, PACK, CHUNKS // PAIR], F32, name="pixel_squares", tag="pixel_squares"
-        )
+        def turn_step():
+            x = len(turned_so_far)
+            if x >= len(turns):
+                return
+            im, c = turns[x]
+            measured = im is image1 and c >= GRAM1
+            transpose_chunk(im, c)
+            empty_banks(im, c, on_scalar)
+            square_waiting()
+            waiting.append((im, c))
+            if measured:
+                to_square.append((im, c))
+            turned_so_far.append(x)
+
+        def quantise_waiting(keep=0):
+            while len(waiting) > keep:
+                im, c = waiting[0]
+                waiting.remove(waiting[0])
+                quantise_turned(im, c)
+
+        partial = small.tile([P, PACK], F32, tag="partial")
+        sum_last(image0["pixel_squares"][:], partial[:])
+        kept = reorder(partial, by_slot, by_block)
+        partial_by_block = small.tile([P, PACK], F32, tag="partial_by_block")
+        sum_last(kept, partial_by_block[:])
+        turn_step()
+        inverse_norm0 = inverse_root(gram_diagonals(gram, partial_by_block), PACK)
+        spread_pixel_norms(image0, inverse_norm0, by_block)
+        copy_pixel_norms(image0)
 
         def load_next_chunk_of_image1():
             if len(image1["rows"]) < CHUNKS:
                 load_chunk(image1, len(image1["rows"]))
 
-        def scale_chunk_of_image0(c, on_gpsimd):
-            scale_chunk(image0, c, on_gpsimd)
-            load_next_chunk_of_image1()
-
-        def turn_step_of_image1(x):
-            if x < CHUNKS:
-                empty_banks(image1, x, image1["banks"], copies)
-            if x + 1 < CHUNKS:
-                image1["banks"] = transpose_chunk(image1, x + 1)
-            if PAIR <= x < CHUNKS + PAIR:
-                square_pair(image1, x // PAIR - 1, (2 * (x % PAIR), 2 * (x % PAIR) + 1))
-
-        for spare in range(ROW_TILES - CHUNKS):
-            load_next_chunk_of_image1()
-        scale_chunk_of_image0(ROUND - 1, True)
-        image1["banks"] = transpose_chunk(image1, 0)
+        gram = [sim_banks.tile([P, P], F32, name="gram%d" % m, tag="sim") for m in range(PACK)]
+        scale_chunk(image0, ROUND - 1, True)
         for first in range(0, CHUNKS - 1, ROUND):
-            for c in range(first, first + ROUND):
-                if c < first + ROUND - 1:
-                    scale_chunk_of_image0(c, False)
-                if first == 0:
-                    turn_step_of_image1(2 * c)
-                    turn_step_of_image1(2 * c + 1)
-                else:
-                    turn_step_of_image1(c + SHIFT)
-            for x in range(0 if first == 0 else first + SHIFT, min(first + ROUND + SHIFT, CHUNKS)):
-                quantise_turned(image1, x)
+            for c in range(first, first + ROUND - 1):
+                scale_chunk(image0, c, False)
+                for step in range(2):
+                    g = 2 * c + step
+                    if first == 0 and g < GRAM1:
+                        add_to_gram(gram, image1["rows"][g], g == 0, g == GRAM1 - 1)
+                    turn_step()
+            for c in range(ROUND):
+                load_next_chunk_of_image1()
+            quantise_waiting(2)
+            if first == 0:
+                gram_squares = gram_diagonals(gram, None)
+                kept = reorder(gram_squares, by_block, by_slot)
+                sum_last(kept, image1["pixel_squares"][:, :, CHUNKS - GRAM1])
             for c in range(first, first + ROUND):
                 similarity_pass(image0, c)
             if first + 2 * ROUND - 1 < CHUNKS:
-                scale_chunk_of_image0(first + 2 * ROUND - 1, True)
-        scale_chunk_of_image0(CHUNKS - 1, False)
-        inverse_norm1 = inverse_root(summed_squares(image1), PACK)
+                scale_chunk(image0, first + 2 * ROUND - 1, True)
+        while len(turned_so_far) <= last_measured:
+            turn_step()
+        square_waiting()
+        scale_chunk(image0, CHUNKS - 1, False)
+        squared_norm1 = small.tile([P, PACK], F32, tag="squared_norm1")
+        sum_last(image1["pixel_squares"][:], squared_norm1[:])
+        inverse_norm1 = inverse_root(squared_norm1, PACK)
+        quantise_waiting()
         similarity_pass(image0, CHUNKS - 1)
-        spread_pixel_norms(
-            image1,
-            inverse_norm1,
-            lambda spread, t: spread[:].rearrange("p (q t) -> p q t", t=PACK)[:, :, t],
-        )
+        spread_pixel_norms(image1, inverse_norm1, by_slot)
+        copy_pixel_norms(image1)
 
-        scale_chunk(image1, ROUND_ALONE - 1, True)
+        scale_chunk(image1, ROUND - 1, True)
         burst_weights(image0)
-        for first in range(0, CHUNKS, ROUND_ALONE):
-            members = range(first, first + ROUND_ALONE)
-            for c in range(first, first + ROUND_ALONE - 1):
+        aggregated = []
+        for first in range(0, CHUNKS - 1, ROUND):
+            members = range(first, first + ROUND)
+            turn_step()
+            for c in range(first, first + ROUND - 1):
                 scale_chunk(image1, c, False)
             if first == 0:
                 weighted_assignment(image0)
+            quantise_waiting(1)
             for c in members:
                 similarity_pass(image1, c)
-            if first + 2 * ROUND_ALONE - 1 < CHUNKS:
-                scale_chunk(image1, first + 2 * ROUND_ALONE - 1, True)
-            for c in members:
-                if c < HALF:
-                    square_aggregate(image0, 2 * c)
-                    square_aggregate(image0, 2 * c + 1)
-            if HALF - 1 + ROUND_ALONE in members:
+            if first == 4 * ROUND:
                 cluster_norms(image0)
+            if first + 2 * ROUND - 1 < CHUNKS:
+                scale_chunk(image1, first + 2 * ROUND - 1, True)
+            for k in range(5):
+                if len(aggregated) < CHUNKS:
+                    square_aggregate(image0, len(aggregated))
+                    aggregated.append(k)
+        scale_chunk(image1, CHUNKS - 1, False)
+        quantise_waiting()
+        similarity_pass(image1, CHUNKS - 1)
 
         burst_weights(image1)
         fetch_cluster_norms(image0)

@@ -26,8 +26,13 @@ EPS_NORM_SQUARED = 1e-24
 EPS_DENOM = 1e-6
 ROW_TILES = 21
 EARLY = 7
-SQUARED0 = 6
-GRAM1 = 3
+SQUARED0 = 8
+GRAM1 = 5
+TURNS_BEHIND = 1
+SS = 4
+VSQ = 6
+N1 = 9
+NV = 4
 ROUND = 3
 ROUND_ALONE = 4
 
@@ -42,7 +47,7 @@ def tile_salad_pa_k_kernel(tc, f_clu, h_score, W_s2, b_s2, burst_par, out):
         turned_pool = ctx.enter_context(tc.tile_pool(name="turned", bufs=6))
         image_pool = ctx.enter_context(tc.tile_pool(name="image", bufs=IMAGES))
         pass_pool = ctx.enter_context(tc.tile_pool(name="pass", bufs=3))
-        codes_pool = ctx.enter_context(tc.tile_pool(name="codes", bufs=4))
+        codes_pool = ctx.enter_context(tc.tile_pool(name="codes", bufs=5))
         gpsimd_pool = ctx.enter_context(tc.tile_pool(name="gpsimd", bufs=1))
         unread_pool = ctx.enter_context(tc.tile_pool(name="unread", bufs=2))
         small = ctx.enter_context(tc.tile_pool(name="small", bufs=2))
@@ -70,7 +75,7 @@ def tile_salad_pa_k_kernel(tc, f_clu, h_score, W_s2, b_s2, burst_par, out):
         nc.vector.memset(minus_half[:], -0.5)
 
         def load_rows(dram_rows):
-            rows = rows_pool.tile([P, PACK, N_PIX], BF16, tag="rows")
+            rows = rows_pool.tile([P, PACK, N_PIX], BF16, tag="rows", align_bytes=64)
             nc.sync.dma_start(out=rows[:], in_=dram_rows.rearrange("(p j) n -> p j n", j=PACK))
             return rows
 
@@ -145,8 +150,10 @@ def tile_salad_pa_k_kernel(tc, f_clu, h_score, W_s2, b_s2, burst_par, out):
                     [P, D_FEAT], U8, name="fT_scales", tag="fT_scales", align_bytes=64
                 ),
                 "cluster_squares": small.tile(
-                    [P, CHUNKS], F32, name="cluster_squares", tag="cluster_squares"
+                    [P, 2 * CHUNKS], F32, name="cluster_squares", tag="cluster_squares"
                 ),
+                "sums": 0,
+                "measured_sums": 0,
             }
 
         def load_chunk(im, c):
@@ -309,12 +316,53 @@ def tile_salad_pa_k_kernel(tc, f_clu, h_score, W_s2, b_s2, burst_par, out):
             )
             im["scaled"][c] = grouped
 
-        def similarity_pass(im, c):
-            if c == 0:
+        def rescale_chunk(im, c):
+            scaled = rows_pool.tile([P, PACK, K_PASS], BF16, tag="rows", align_bytes=64)
+            for t in range(PACK):
+                nc.scalar.activation(
+                    out=scaled[:, t, :].rearrange("q (v p e) -> q v p e", v=2, e=2),
+                    in_=im["turned"][c][:, :, t].rearrange("q (v e p) -> q v p e", v=2, e=2),
+                    func=ACT.Copy,
+                    scale=im["inverse_norm"][:, t : t + 1],
+                )
+            im["rescaled"] = scaled
+
+        def turn_back(im, c):
+            words = im["rescaled"][:].bitcast(F32)
+            grouped = rows_pool.tile([P, N_PIX, PACK], BF16, tag="rows", align_bytes=64)
+            grouped_words = grouped[:].bitcast(F32)
+            for half in range(2):
+                bank = banks.tile([P, 2, 2, P], F32, name="turned_bank", tag="bank")
+                for tt in range(2):
+                    for v in range(2):
+                        nc.tensor.transpose(
+                            bank[:, tt, v, :], words[:, 2 * half + tt, v * P : (v + 1) * P], ident[:]
+                        )
+                nc.scalar.copy(
+                    out=grouped_words[:, half * 2 * P : (half + 1) * 2 * P, :].rearrange(
+                        "p (tt q) v -> p tt q v", tt=2
+                    ),
+                    in_=bank[:].rearrange("p tt v q -> p tt q v"),
+                )
+            im["scaled"][c] = grouped
+
+        passes = []
+        quantised = []
+
+        def quantise_scaled(im, c):
+            quantised.append((im, c, quantise_pass(im["scaled"][c])))
+
+        def similarity_pass():
+            if not quantised:
+                return
+            im, c, (fn_codes, fn_scales) = quantised[0]
+            quantised.remove(quantised[0])
+            n = len(passes) % CHUNKS
+            passes.append(c)
+            if n == 0:
                 im["sim"] = [
                     sim_banks.tile([P, N_PIX], F32, name="sim%d" % t, tag="sim") for t in range(PACK)
                 ]
-            fn_codes, fn_scales = quantise_pass(im["scaled"][c])
             for t in range(PACK):
                 nc.tensor.matmul_mx(
                     out=im["sim"][t][:],
@@ -322,9 +370,13 @@ def tile_salad_pa_k_kernel(tc, f_clu, h_score, W_s2, b_s2, burst_par, out):
                     lhsT_scale=fn_scales[:, t * P : (t + 1) * P],
                     rhs=fn_codes[:].bitcast(FP8X4),
                     rhs_scale=fn_scales[:],
-                    start=(c == 0),
-                    stop=(c == CHUNKS - 1),
+                    start=(n == 0),
+                    stop=(n == CHUNKS - 1),
                 )
+
+        def similarity_rest():
+            while quantised:
+                similarity_pass()
 
         def burst_weights(im):
             w = small.tile([P, PACK], F32, tag="w")
@@ -361,9 +413,10 @@ def tile_salad_pa_k_kernel(tc, f_clu, h_score, W_s2, b_s2, burst_par, out):
             im["pm_codes"] = pm_codes
             im["pm_scales"] = pm_scales
 
-        def square_aggregate(im, c):
+        def turned_aggregate(im, c):
             columns = slice(c * K_PASS, (c + 1) * K_PASS)
-            v_turned = banks.tile([P, K_PASS], F32, tag="bank")
+            pool, tag = (banks, "bank") if im["index"] == 0 else (sim_banks, "sim")
+            v_turned = pool.tile([P, K_PASS], F32, name="v_turned", tag=tag)
             nc.tensor.matmul_mx(
                 out=v_turned[:],
                 lhsT=im["pm_codes"][:].bitcast(FP8X4),
@@ -373,18 +426,52 @@ def tile_salad_pa_k_kernel(tc, f_clu, h_score, W_s2, b_s2, burst_par, out):
                 start=True,
                 stop=True,
             )
+            return v_turned
+
+        def square_aggregate(im, c):
+            v_turned = turned_aggregate(im, c)
             unread = unread_pool.tile([P, K_PASS], BF16, tag="bank_wide")
+            n = im["sums"]
             nc.scalar.activation(
                 out=unread[:],
                 in_=v_turned[:],
                 func=ACT.Square,
-                accum_out=im["cluster_squares"][:, c : c + 1],
+                accum_out=im["cluster_squares"][:, n : n + 1],
             )
+            im["sums"] += 1
+
+        def measure_aggregate(im, c):
+            v_turned = turned_aggregate(im, c)
+            n = im["measured_sums"]
+            nc.vector.bn_stats(
+                out=im["stats"][:, n, :, :].rearrange("p h s -> p (h s)"), in_=v_turned[:]
+            )
+            im["measured_sums"] += 1
+
+        def squares_from_stats(im):
+            n, first = im["measured_sums"], im["sums"]
+            stats = im["stats"][:, 0:n, :, :].rearrange("p n h s -> p (n h) s")
+            mean_squared = small.tile([P, 2 * n], F32, name="mean_squared", tag="mean_squared")
+            nc.vector.scalar_tensor_tensor(
+                out=mean_squared[:],
+                in0=stats[:, :, 1],
+                scalar=float(K_PASS // 2),
+                in1=stats[:, :, 1],
+                op0=ALU.mult,
+                op1=ALU.mult,
+            )
+            nc.vector.tensor_tensor(
+                out=im["cluster_squares"][:, first : first + 2 * n],
+                in0=mean_squared[:],
+                in1=stats[:, :, 2],
+                op=ALU.add,
+            )
+            im["sums"] += 2 * n
 
         def cluster_norms(im):
             squared_norm = small.tile([P, 1], F32, tag="v_squared_norm")
             nc.vector.tensor_reduce(
-                out=squared_norm[:], in_=im["cluster_squares"][:], axis=AXIS.X, op=ALU.add
+                out=squared_norm[:], in_=im["cluster_squares"][:, 0 : im["sums"]], axis=AXIS.X, op=ALU.add
             )
             inverse_norm = inverse_root(squared_norm, 1)
             spread_bank = banks.tile([P, K_CLU], F32, tag="bank")
@@ -397,7 +484,8 @@ def tile_salad_pa_k_kernel(tc, f_clu, h_score, W_s2, b_s2, burst_par, out):
             im["v_spread"] = v_spread
 
         def output_chunk(im, c):
-            v = banks.tile([P, PACK, K_CLU], F32, tag="bank")
+            pool, tag = (banks, "bank") if im["index"] == 0 or c % 2 == 0 else (sim_banks, "sim")
+            v = pool.tile([P, PACK, K_CLU], F32, name="v", tag=tag)
             for j in range(PACK):
                 columns = slice(c * K_PASS + j * P, c * K_PASS + (j + 1) * P)
                 nc.tensor.matmul_mx(
@@ -409,7 +497,7 @@ def tile_salad_pa_k_kernel(tc, f_clu, h_score, W_s2, b_s2, burst_par, out):
                     start=True,
                     stop=True,
                 )
-            normed = rows_pool.tile([P, PACK, K_CLU], F32, tag="rows")
+            normed = rows_pool.tile([P, PACK, K_CLU], F32, tag="rows", align_bytes=64)
             nc.vector.tensor_tensor(
                 out=normed[:],
                 in0=v[:],
@@ -468,15 +556,8 @@ def tile_salad_pa_k_kernel(tc, f_clu, h_score, W_s2, b_s2, burst_par, out):
                 soft_assignment(image1)
         rest0 = [(image0, c) for c in range(SQUARED0, CHUNKS)]
         rest1 = [(image1, c) for c in range(GRAM1, CHUNKS)]
-        pattern = [0, 1, 0, 1, 0] + 4 * [1, 0, 1, 1] + [0] * 16
-        turns = []
-        for which in pattern:
-            source = rest1 if which else rest0
-            if source:
-                turns.append(source[0])
-                source.remove(source[0])
-        turns += rest0 + rest1 + [(image1, c) for c in range(GRAM1)]
-        last_measured = turns.index((image1, CHUNKS - 1))
+        turns = rest0[:4] + rest1 + [(image1, GRAM1 - 1)]
+        by_vector = rest0[4:]
         turned_so_far = []
         waiting = []
         to_square = []
@@ -487,18 +568,17 @@ def tile_salad_pa_k_kernel(tc, f_clu, h_score, W_s2, b_s2, burst_par, out):
             to_square.clear()
 
         def turn_step():
-            x = len(turned_so_far)
-            if x >= len(turns):
+            if not turns:
                 return
-            im, c = turns[x]
-            measured = im is image1 and c >= GRAM1
+            im, c = turns[0]
+            turns.remove(turns[0])
             transpose_chunk(im, c)
             empty_banks(im, c, on_scalar)
             square_waiting()
             waiting.append((im, c))
-            if measured:
+            if im is image1 and c >= GRAM1:
                 to_square.append((im, c))
-            turned_so_far.append(x)
+            turned_so_far.append(c)
 
         def quantise_waiting(keep=0):
             while len(waiting) > keep:
@@ -511,6 +591,7 @@ def tile_salad_pa_k_kernel(tc, f_clu, h_score, W_s2, b_s2, burst_par, out):
         kept = reorder(partial, by_slot, by_block)
         partial_by_block = small.tile([P, PACK], F32, tag="partial_by_block")
         sum_last(kept, partial_by_block[:])
+        turn_step()
         turn_step()
         inverse_norm0 = inverse_root(gram_diagonals(gram, partial_by_block), PACK)
         spread_pixel_norms(image0, inverse_norm0, by_block)
@@ -526,67 +607,112 @@ def tile_salad_pa_k_kernel(tc, f_clu, h_score, W_s2, b_s2, burst_par, out):
             for c in range(first, first + ROUND - 1):
                 scale_chunk(image0, c, False)
                 for step in range(2):
-                    g = 2 * c + step
-                    if first == 0 and g < GRAM1:
+                    g = 2 * (c - first) + step
+                    if first == 0:
                         add_to_gram(gram, image1["rows"][g], g == 0, g == GRAM1 - 1)
-                    turn_step()
+                        if g % 2 == 1:
+                            turn_step()
+                    elif g < 3:
+                        turn_step()
+                        similarity_pass()
+            if first == 0:
+                add_to_gram(gram, image1["rows"][4], False, True)
             for c in range(ROUND):
                 load_next_chunk_of_image1()
-            quantise_waiting(2)
+            if by_vector:
+                im, v = by_vector[0]
+                by_vector.remove(by_vector[0])
+                transpose_chunk(im, v)
+            else:
+                v = None
+            quantise_waiting(TURNS_BEHIND)
             if first == 0:
                 gram_squares = gram_diagonals(gram, None)
                 kept = reorder(gram_squares, by_block, by_slot)
                 sum_last(kept, image1["pixel_squares"][:, :, CHUNKS - GRAM1])
             for c in range(first, first + ROUND):
-                similarity_pass(image0, c)
+                quantise_scaled(image0, c)
+            if v is not None:
+                empty_banks(im, v, on_vector)
+                waiting.append((im, v))
             if first + 2 * ROUND - 1 < CHUNKS:
                 scale_chunk(image0, first + 2 * ROUND - 1, True)
-        while len(turned_so_far) <= last_measured:
+        while turns:
             turn_step()
         square_waiting()
+        turns += by_vector + [(image1, c) for c in range(GRAM1 - 1)]
         scale_chunk(image0, CHUNKS - 1, False)
         squared_norm1 = small.tile([P, PACK], F32, tag="squared_norm1")
         sum_last(image1["pixel_squares"][:], squared_norm1[:])
         inverse_norm1 = inverse_root(squared_norm1, PACK)
+        similarity_rest()
         quantise_waiting()
-        similarity_pass(image0, CHUNKS - 1)
+        quantise_scaled(image0, CHUNKS - 1)
+        similarity_rest()
         spread_pixel_norms(image1, inverse_norm1, by_slot)
         copy_pixel_norms(image1)
 
-        scale_chunk(image1, ROUND - 1, True)
+        image1["inverse_norm"] = inverse_norm1
+        whole = [c for c in range(CHUNKS) if c >= SS]
+        first_gpsimd = whole[2]
+        scale_chunk(image1, first_gpsimd, True)
         burst_weights(image0)
         aggregated = []
-        for first in range(0, CHUNKS - 1, ROUND):
-            members = range(first, first + ROUND)
-            turn_step()
-            for c in range(first, first + ROUND - 1):
+        ready = []
+        rounds = -(-len(whole) // ROUND)
+        for r in range(rounds):
+            members = whole[r * ROUND : (r + 1) * ROUND]
+            for k, c in enumerate(members[:2]):
                 scale_chunk(image1, c, False)
-            if first == 0:
+                if k == 0:
+                    turn_step()
+                    if r < SS:
+                        rescale_chunk(image1, r)
+                similarity_pass()
+            similarity_pass()
+            if r < SS:
+                turn_back(image1, r)
+            similarity_pass()
+            if r == 0:
                 weighted_assignment(image0)
-            quantise_waiting(1)
-            for c in members:
-                similarity_pass(image1, c)
-            if first == 4 * ROUND:
-                cluster_norms(image0)
-            if first + 2 * ROUND - 1 < CHUNKS:
-                scale_chunk(image1, first + 2 * ROUND - 1, True)
-            for k in range(5):
+            for k in range(VSQ if r > 0 else 0):
                 if len(aggregated) < CHUNKS:
                     square_aggregate(image0, len(aggregated))
                     aggregated.append(k)
-        scale_chunk(image1, CHUNKS - 1, False)
-        quantise_waiting()
-        similarity_pass(image1, CHUNKS - 1)
+            quantise_waiting(0)
+            for c in ready:
+                quantise_scaled(image1, c)
+            ready = [r] if r < SS else []
+            for c in members:
+                quantise_scaled(image1, c)
+            similarity_pass()
+            if r == rounds - 1:
+                similarity_rest()
+            if (r + 1) * ROUND + 2 < len(whole):
+                scale_chunk(image1, whole[(r + 1) * ROUND + 2], True)
+        for c in ready:
+            quantise_scaled(image1, c)
+        similarity_rest()
+        cluster_norms(image0)
 
         burst_weights(image1)
         fetch_cluster_norms(image0)
-        for c in range(HALF):
+        for c in range(N1):
             output_chunk(image0, c)
         weighted_assignment(image1)
+        later = list(range(N1, CHUNKS))
+        image1["stats"] = small.tile([P, NV, 2, 3], F32, name="stats", tag="stats")
         for c in range(CHUNKS):
-            square_aggregate(image1, c)
-            if c < HALF:
-                output_chunk(image0, HALF + c)
+            if c % 3 == 2 and image1["measured_sums"] < NV:
+                measure_aggregate(image1, c)
+            else:
+                square_aggregate(image1, c)
+                if later and c % 2 == 0:
+                    output_chunk(image0, later[0])
+                    later.remove(later[0])
+        squares_from_stats(image1)
+        for c in later:
+            output_chunk(image0, c)
         cluster_norms(image1)
         fetch_cluster_norms(image1)
         for c in range(CHUNKS):

@@ -25,16 +25,19 @@ HALF = CHUNKS // 2
 EPS_NORM_SQUARED = 1e-24
 EPS_DENOM = 1e-6
 ROW_TILES = 21
-EARLY = 7
-SQUARED0 = 8
-GRAM1 = 5
+EARLY = 9
+SQUARED0 = 7
 TURNS_BEHIND = 1
+PARAMETERS_AT = 7
+HIDDEN_AT = (9, 13)
+EXP_AT = 3
+STEPS = 3
+VSTEP = (0, 1, 0, 1, 0)
 SS = 4
 VSQ = 6
 N1 = 9
 NV = 4
 ROUND = 3
-ROUND_ALONE = 4
 
 FLOPS = 2 * IMAGES * (K_CLU * F_HID * N_PIX + N_PIX * D_FEAT * N_PIX + D_FEAT * N_PIX * K_CLU)
 
@@ -206,9 +209,9 @@ def tile_salad_pa_k_kernel(tc, f_clu, h_score, W_s2, b_s2, burst_par, out):
             nc.vector.tensor_copy(out=columns_by_slot(h_grouped), in_=pixels_by_slot(im["h_rows"]))
             im["h"] = quantise_pass(h_grouped)
 
-        def soft_assignment(im):
+        def score_pixels(im):
             h_codes, h_scales = im["h"]
-            product = banks.tile([P, PACK, K_CLU], F32, tag="bank")
+            product = banks.tile([P, PACK, K_CLU], F32, name="product", tag="bank")
             for t in range(PACK):
                 nc.tensor.matmul_mx(
                     out=product[:, t, :],
@@ -219,28 +222,31 @@ def tile_salad_pa_k_kernel(tc, f_clu, h_score, W_s2, b_s2, burst_par, out):
                     start=True,
                     stop=True,
                 )
-            expo = image_pool.tile([P, PACK, K_CLU], F32, tag="expo")
-            nc.vector.tensor_tensor(
-                out=expo[:],
+            im["expo"] = image_pool.tile([P, PACK, K_CLU], F32, name="expo", tag="expo")
+            nc.vector.scalar_tensor_tensor(
+                out=im["expo"][:],
                 in0=product[:],
+                scalar=-1.0,
                 in1=held[:, 0:K_CLU].unsqueeze(1).to_broadcast([P, PACK, K_CLU]),
-                op=ALU.add,
+                op0=ALU.mult,
+                op1=ALU.subtract,
             )
-            top = small.tile([P, PACK], F32, tag="top")
-            nc.vector.tensor_reduce(out=top[:], in_=expo[:], axis=AXIS.X, op=ALU.max)
-            minus_top = small.tile([P, PACK], F32, tag="minus_top")
-            nc.vector.tensor_scalar_mul(out=minus_top[:], in0=top[:], scalar1=-1.0)
-            expo_sum = image_pool.tile([P, PACK], F32, tag="expo_sum")
+            im["least"] = small.tile([P, PACK], F32, name="least", tag="least")
+            nc.vector.tensor_reduce(
+                out=im["least"][:], in_=im["expo"][:], axis=AXIS.X, op=ALU.min
+            )
+
+        def exponentiate(im):
+            im["expo_sum"] = image_pool.tile([P, PACK], F32, name="expo_sum", tag="expo_sum")
             for t in range(PACK):
                 nc.scalar.activation(
-                    out=expo[:, t, :],
-                    in_=expo[:, t, :],
+                    out=im["expo"][:, t, :],
+                    in_=im["expo"][:, t, :],
                     func=ACT.Exp,
-                    bias=minus_top[:, t : t + 1],
-                    accum_out=expo_sum[:, t : t + 1],
+                    scale=-1.0,
+                    bias=im["least"][:, t : t + 1],
+                    accum_out=im["expo_sum"][:, t : t + 1],
                 )
-            im["expo"] = expo
-            im["expo_sum"] = expo_sum
 
         def add_to_gram(gram, rows, first, last):
             for j in range(PACK):
@@ -254,18 +260,20 @@ def tile_salad_pa_k_kernel(tc, f_clu, h_score, W_s2, b_s2, burst_par, out):
                         stop=(last and j == PACK - 1),
                     )
 
-        def gram_diagonals(gram, extra):
-            width = P + (0 if extra is None else 1)
-            on_diagonal = const.tile([P, PACK, P + PACK], F32, tag="on_diagonal")
+        def diagonal_sums(blocks):
+            sums = small.tile([P, PACK], F32, name="diagonal_sums", tag="diagonal_sums")
             for m in range(PACK):
-                nc.vector.tensor_tensor(
-                    out=on_diagonal[:, m, 0:P], in0=gram[m][:], in1=ident[:], op=ALU.mult
+                unread = unread_pool.tile([P, P], F32, name="unread", tag="masked")
+                nc.vector.scalar_tensor_tensor(
+                    out=unread[:],
+                    in0=blocks[m],
+                    scalar=1.0,
+                    in1=ident[:],
+                    op0=ALU.mult,
+                    op1=ALU.mult,
+                    accum_out=sums[:, m : m + 1],
                 )
-            if extra is not None:
-                nc.vector.tensor_copy(out=on_diagonal[:, :, P], in_=extra[:])
-            squares = small.tile([P, PACK], F32, tag="gram_squares")
-            nc.vector.tensor_reduce(out=squares[:], in_=on_diagonal[:, :, 0:width], axis=AXIS.X, op=ALU.add)
-            return squares
+            return sums
 
         def by_block(bank):
             return bank[:].rearrange("p (m i) -> p m i", m=PACK)
@@ -276,14 +284,7 @@ def tile_salad_pa_k_kernel(tc, f_clu, h_score, W_s2, b_s2, burst_par, out):
         def reorder(per_pixel, source, target):
             spread = banks.tile([P, N_PIX], F32, name="reorder_bank", tag="bank")
             spread_over_partitions([source(spread)[:, k, :] for k in range(PACK)], per_pixel)
-            kept = const.tile([P, PACK, P + PACK], F32, tag="on_diagonal")
-            nc.vector.tensor_tensor(
-                out=kept[:, :, 0:P],
-                in0=target(spread),
-                in1=ident[:].unsqueeze(1).to_broadcast([P, PACK, P]),
-                op=ALU.mult,
-            )
-            return kept[:, :, 0:P]
+            return diagonal_sums([target(spread)[:, k, :] for k in range(PACK)])
 
         def sum_last(values, out):
             nc.vector.tensor_reduce(out=out, in_=values, axis=AXIS.X, op=ALU.add)
@@ -396,8 +397,14 @@ def tile_salad_pa_k_kernel(tc, f_clu, h_score, W_s2, b_s2, burst_par, out):
 
         def weighted_assignment(im):
             divisor = small.tile([P, PACK], F32, tag="divisor")
-            nc.vector.tensor_scalar_add(out=divisor[:], in0=im["w_power"][:], scalar1=EPS_DENOM)
-            nc.vector.tensor_mul(out=divisor[:], in0=divisor[:], in1=im["expo_sum"][:])
+            nc.vector.scalar_tensor_tensor(
+                out=divisor[:],
+                in0=im["w_power"][:],
+                scalar=EPS_DENOM,
+                in1=im["expo_sum"][:],
+                op0=ALU.add,
+                op1=ALU.mult,
+            )
             share = small.tile([P, PACK], F32, tag="share")
             nc.vector.reciprocal(out=share[:], in_=divisor[:])
             pm_grouped = small.tile([P, K_CLU, PACK], BF16, tag="pm_grouped", align_bytes=64)
@@ -513,7 +520,7 @@ def tile_salad_pa_k_kernel(tc, f_clu, h_score, W_s2, b_s2, burst_par, out):
 
         image0 = new_image(0)
         image1 = new_image(1)
-        for im, slots in ((image0, SQUARED0), (image1, CHUNKS - GRAM1 + 1)):
+        for im, slots in ((image0, SQUARED0), (image1, CHUNKS)):
             im["measured"] = 0
             im["pixel_squares"] = small.tile(
                 [P, PACK, slots], F32, name="pixel_squares", tag="pixel_squares%d" % im["index"]
@@ -532,33 +539,30 @@ def tile_salad_pa_k_kernel(tc, f_clu, h_score, W_s2, b_s2, burst_par, out):
         on_vector = (nc.vector.tensor_copy, nc.vector.tensor_copy)
         on_both = (nc.scalar.copy, nc.vector.tensor_copy)
 
+        gram = [sim_banks.tile([P, P], F32, name="gram%d" % m, tag="sim") for m in range(PACK)]
+        squared = [2 * k for k in range(SQUARED0)]
+        others = [c for c in range(CHUNKS) if c not in squared]
         for c in range(CHUNKS):
-            if c == SQUARED0:
-                gram = [sim_banks.tile([P, P], F32, name="gram%d" % m, tag="sim") for m in range(PACK)]
-            if c < SQUARED0:
-                transpose_chunk(image0, c, ((sim_banks, "sim"), (sim_banks, "sim")) if c % 2 == 0 else None)
+            if c in squared:
+                transpose_chunk(image0, c)
+                empty_banks(image0, c, on_vector)
+                square_chunk(image0, c)
+                if c > 0:
+                    quantise_turned(image0, c - 2)
             else:
-                add_to_gram(gram, image0["rows"][c], c == SQUARED0, c == CHUNKS - 1)
-            if 1 <= c <= SQUARED0:
-                empty_banks(image0, c - 1, on_vector)
-                square_chunk(image0, c - 1)
-            if 2 <= c <= SQUARED0 + 1:
-                quantise_turned(image0, c - 2)
-            if c == SQUARED0 + 1:
+                add_to_gram(gram, image0["rows"][c], c == others[0], c == others[-1])
+            if c == PARAMETERS_AT:
                 held, exponent = fetch_parameters()
                 w_codes, w_scales = quantise_w()
-                quantise_hidden(image0)
-                quantise_hidden(image1)
-                for c1 in range(IMAGES):
-                    load_chunk(image1, len(image1["rows"]))
-            if c == SQUARED0 + 5:
-                soft_assignment(image0)
-                soft_assignment(image1)
-        rest0 = [(image0, c) for c in range(SQUARED0, CHUNKS)]
-        rest1 = [(image1, c) for c in range(GRAM1, CHUNKS)]
-        turns = rest0[:4] + rest1 + [(image1, GRAM1 - 1)]
-        by_vector = rest0[4:]
-        turned_so_far = []
+            if c in HIDDEN_AT:
+                im = (image0, image1)[HIDDEN_AT.index(c)]
+                quantise_hidden(im)
+                load_chunk(image1, len(image1["rows"]))
+        quantise_turned(image0, squared[-1])
+
+        rest0 = [(image0, c) for c in others]
+        rest1 = [(image1, c) for c in range(CHUNKS)]
+
         waiting = []
         to_square = []
 
@@ -567,18 +571,17 @@ def tile_salad_pa_k_kernel(tc, f_clu, h_score, W_s2, b_s2, burst_par, out):
                 square_chunk(im, c)
             to_square.clear()
 
-        def turn_step():
-            if not turns:
+        def turn_step(rest, copies):
+            if not rest:
                 return
-            im, c = turns[0]
-            turns.remove(turns[0])
+            im, c = rest[0]
+            rest.remove(rest[0])
             transpose_chunk(im, c)
-            empty_banks(im, c, on_scalar)
+            empty_banks(im, c, copies)
             square_waiting()
             waiting.append((im, c))
-            if im is image1 and c >= GRAM1:
+            if im is image1:
                 to_square.append((im, c))
-            turned_so_far.append(c)
 
         def quantise_waiting(keep=0):
             while len(waiting) > keep:
@@ -588,12 +591,17 @@ def tile_salad_pa_k_kernel(tc, f_clu, h_score, W_s2, b_s2, burst_par, out):
 
         partial = small.tile([P, PACK], F32, tag="partial")
         sum_last(image0["pixel_squares"][:], partial[:])
-        kept = reorder(partial, by_slot, by_block)
-        partial_by_block = small.tile([P, PACK], F32, tag="partial_by_block")
-        sum_last(kept, partial_by_block[:])
-        turn_step()
-        turn_step()
-        inverse_norm0 = inverse_root(gram_diagonals(gram, partial_by_block), PACK)
+        partial_by_block = reorder(partial, by_slot, by_block)
+        turn_step(rest0, on_scalar)
+        turn_step(rest0, on_scalar)
+        squared_norm0 = small.tile([P, PACK], F32, tag="squared_norm0")
+        nc.vector.tensor_tensor(
+            out=squared_norm0[:],
+            in0=diagonal_sums([block[:] for block in gram])[:],
+            in1=partial_by_block[:],
+            op=ALU.add,
+        )
+        inverse_norm0 = inverse_root(squared_norm0, PACK)
         spread_pixel_norms(image0, inverse_norm0, by_block)
         copy_pixel_norms(image0)
 
@@ -601,97 +609,85 @@ def tile_salad_pa_k_kernel(tc, f_clu, h_score, W_s2, b_s2, burst_par, out):
             if len(image1["rows"]) < CHUNKS:
                 load_chunk(image1, len(image1["rows"]))
 
-        gram = [sim_banks.tile([P, P], F32, name="gram%d" % m, tag="sim") for m in range(PACK)]
-        scale_chunk(image0, ROUND - 1, True)
+        order0 = squared + others
+        scale_chunk(image0, order0[ROUND - 1], True)
         for first in range(0, CHUNKS - 1, ROUND):
-            for c in range(first, first + ROUND - 1):
-                scale_chunk(image0, c, False)
+            for k in range(ROUND - 1):
+                scale_chunk(image0, order0[first + k], False)
+                if first == 0:
+                    score_pixels((image0, image1)[k])
+                if first == EXP_AT:
+                    exponentiate((image0, image1)[k])
                 for step in range(2):
-                    g = 2 * (c - first) + step
-                    if first == 0:
-                        add_to_gram(gram, image1["rows"][g], g == 0, g == GRAM1 - 1)
-                        if g % 2 == 1:
-                            turn_step()
-                    elif g < 3:
-                        turn_step()
+                    if 2 * k + step < STEPS:
+                        turn_step(rest1, on_scalar)
                         similarity_pass()
-            if first == 0:
-                add_to_gram(gram, image1["rows"][4], False, True)
             for c in range(ROUND):
                 load_next_chunk_of_image1()
-            if by_vector:
-                im, v = by_vector[0]
-                by_vector.remove(by_vector[0])
-                transpose_chunk(im, v)
-            else:
-                v = None
+            source = (rest0, rest1)[VSTEP[first // ROUND]]
+            im, v = source[0]
+            source.remove(source[0])
+            transpose_chunk(im, v)
             quantise_waiting(TURNS_BEHIND)
-            if first == 0:
-                gram_squares = gram_diagonals(gram, None)
-                kept = reorder(gram_squares, by_block, by_slot)
-                sum_last(kept, image1["pixel_squares"][:, :, CHUNKS - GRAM1])
-            for c in range(first, first + ROUND):
-                quantise_scaled(image0, c)
-            if v is not None:
-                empty_banks(im, v, on_vector)
-                waiting.append((im, v))
+            for k in range(ROUND):
+                quantise_scaled(image0, order0[first + k])
+            empty_banks(im, v, on_vector)
+            waiting.append((im, v))
+            if im is image1:
+                to_square.append((im, v))
             if first + 2 * ROUND - 1 < CHUNKS:
-                scale_chunk(image0, first + 2 * ROUND - 1, True)
-        while turns:
-            turn_step()
+                scale_chunk(image0, order0[first + 2 * ROUND - 1], True)
+        while rest1:
+            turn_step(rest1, on_scalar)
         square_waiting()
-        turns += by_vector + [(image1, c) for c in range(GRAM1 - 1)]
-        scale_chunk(image0, CHUNKS - 1, False)
+        scale_chunk(image0, order0[CHUNKS - 1], False)
         squared_norm1 = small.tile([P, PACK], F32, tag="squared_norm1")
         sum_last(image1["pixel_squares"][:], squared_norm1[:])
         inverse_norm1 = inverse_root(squared_norm1, PACK)
         similarity_rest()
         quantise_waiting()
-        quantise_scaled(image0, CHUNKS - 1)
+        quantise_scaled(image0, order0[CHUNKS - 1])
         similarity_rest()
+        image1["inverse_norm"] = inverse_norm1
+        whole = list(range(CHUNKS - SS))
+        rescaled = list(range(CHUNKS - SS, CHUNKS))
+        rescale_chunk(image1, rescaled[0])
         spread_pixel_norms(image1, inverse_norm1, by_slot)
         copy_pixel_norms(image1)
 
-        image1["inverse_norm"] = inverse_norm1
-        whole = [c for c in range(CHUNKS) if c >= SS]
-        first_gpsimd = whole[2]
-        scale_chunk(image1, first_gpsimd, True)
+        scale_chunk(image1, whole[ROUND - 1], True)
         burst_weights(image0)
-        aggregated = []
-        ready = []
-        rounds = -(-len(whole) // ROUND)
+        to_aggregate = list(range(CHUNKS))
+
+        def aggregate_step():
+            if to_aggregate:
+                square_aggregate(image0, to_aggregate[0])
+                to_aggregate.remove(to_aggregate[0])
+
+        rounds = len(whole) // ROUND
         for r in range(rounds):
             members = whole[r * ROUND : (r + 1) * ROUND]
-            for k, c in enumerate(members[:2]):
-                scale_chunk(image1, c, False)
-                if k == 0:
-                    turn_step()
-                    if r < SS:
-                        rescale_chunk(image1, r)
+            scale_chunk(image1, members[0], False)
+            for k in range(2):
+                turn_step(rest0, on_scalar)
+            for k in range(2 if r > 0 else 0):
                 similarity_pass()
-            similarity_pass()
-            if r < SS:
-                turn_back(image1, r)
-            similarity_pass()
+                aggregate_step()
+            turn_back(image1, rescaled[r])
+            scale_chunk(image1, members[1], False)
+            if r + 1 < SS:
+                rescale_chunk(image1, rescaled[r + 1])
             if r == 0:
                 weighted_assignment(image0)
-            for k in range(VSQ if r > 0 else 0):
-                if len(aggregated) < CHUNKS:
-                    square_aggregate(image0, len(aggregated))
-                    aggregated.append(k)
-            quantise_waiting(0)
-            for c in ready:
-                quantise_scaled(image1, c)
-            ready = [r] if r < SS else []
+            for k in range(4 if r > 0 else 0):
+                similarity_pass()
+                aggregate_step()
+            quantise_waiting()
+            quantise_scaled(image1, rescaled[r])
             for c in members:
                 quantise_scaled(image1, c)
-            similarity_pass()
-            if r == rounds - 1:
-                similarity_rest()
-            if (r + 1) * ROUND + 2 < len(whole):
-                scale_chunk(image1, whole[(r + 1) * ROUND + 2], True)
-        for c in ready:
-            quantise_scaled(image1, c)
+            if (r + 1) * ROUND < len(whole):
+                scale_chunk(image1, whole[(r + 2) * ROUND - 1], True)
         similarity_rest()
         cluster_norms(image0)
 

@@ -25,18 +25,20 @@ HALF = CHUNKS // 2
 EPS_NORM_SQUARED = 1e-24
 EPS_DENOM = 1e-6
 ROW_TILES = 21
-EARLY = 9
+EARLY = 13
 SQUARED0 = 7
 TURNS_BEHIND = 1
 PARAMETERS_AT = 7
-HIDDEN_AT = (9, 13)
+HIDDEN_AT = 15
 EXP_AT = 3
 STEPS = 3
-VSTEP = (0, 1, 0, 1, 0)
+VSTEP = (0, 0, 0, 1, 0)
 SS = 4
-VSQ = 6
 N1 = 9
 NV = 4
+NV0 = 2
+A1 = 2
+A2 = 3
 ROUND = 3
 
 FLOPS = 2 * IMAGES * (K_CLU * F_HID * N_PIX + N_PIX * D_FEAT * N_PIX + D_FEAT * N_PIX * K_CLU)
@@ -157,6 +159,7 @@ def tile_salad_pa_k_kernel(tc, f_clu, h_score, W_s2, b_s2, burst_par, out):
                 ),
                 "sums": 0,
                 "measured_sums": 0,
+                "stats": small.tile([P, CHUNKS // 2, 2, 3], F32, name="stats", tag="stats"),
             }
 
         def load_chunk(im, c):
@@ -529,9 +532,9 @@ def tile_salad_pa_k_kernel(tc, f_clu, h_score, W_s2, b_s2, burst_par, out):
         for c in range(EARLY):
             load_chunk(image0, c)
         load_hidden(image0)
-        load_hidden(image1)
         for c in range(EARLY, CHUNKS):
             load_chunk(image0, c)
+        load_hidden(image1)
         for c in range(ROW_TILES - CHUNKS - IMAGES):
             load_chunk(image1, c)
 
@@ -540,7 +543,7 @@ def tile_salad_pa_k_kernel(tc, f_clu, h_score, W_s2, b_s2, burst_par, out):
         on_both = (nc.scalar.copy, nc.vector.tensor_copy)
 
         gram = [sim_banks.tile([P, P], F32, name="gram%d" % m, tag="sim") for m in range(PACK)]
-        squared = [2 * k for k in range(SQUARED0)]
+        squared = [0] + [2 * k + 1 for k in range(SQUARED0 - 1)]
         others = [c for c in range(CHUNKS) if c not in squared]
         for c in range(CHUNKS):
             if c in squared:
@@ -548,15 +551,14 @@ def tile_salad_pa_k_kernel(tc, f_clu, h_score, W_s2, b_s2, burst_par, out):
                 empty_banks(image0, c, on_vector)
                 square_chunk(image0, c)
                 if c > 0:
-                    quantise_turned(image0, c - 2)
+                    quantise_turned(image0, squared[squared.index(c) - 1])
             else:
                 add_to_gram(gram, image0["rows"][c], c == others[0], c == others[-1])
             if c == PARAMETERS_AT:
                 held, exponent = fetch_parameters()
                 w_codes, w_scales = quantise_w()
-            if c in HIDDEN_AT:
-                im = (image0, image1)[HIDDEN_AT.index(c)]
-                quantise_hidden(im)
+            if c == HIDDEN_AT:
+                quantise_hidden(image0)
                 load_chunk(image1, len(image1["rows"]))
         quantise_turned(image0, squared[-1])
 
@@ -614,10 +616,10 @@ def tile_salad_pa_k_kernel(tc, f_clu, h_score, W_s2, b_s2, burst_par, out):
         for first in range(0, CHUNKS - 1, ROUND):
             for k in range(ROUND - 1):
                 scale_chunk(image0, order0[first + k], False)
-                if first == 0:
-                    score_pixels((image0, image1)[k])
-                if first == EXP_AT:
-                    exponentiate((image0, image1)[k])
+                if first == 0 and k == 0:
+                    score_pixels(image0)
+                if first == EXP_AT and k == 0:
+                    exponentiate(image0)
                 for step in range(2):
                     if 2 * k + step < STEPS:
                         turn_step(rest1, on_scalar)
@@ -652,10 +654,13 @@ def tile_salad_pa_k_kernel(tc, f_clu, h_score, W_s2, b_s2, burst_par, out):
         whole = list(range(CHUNKS - SS))
         rescaled = list(range(CHUNKS - SS, CHUNKS))
         rescale_chunk(image1, rescaled[0])
+        quantise_hidden(image1)
         spread_pixel_norms(image1, inverse_norm1, by_slot)
         copy_pixel_norms(image1)
 
         scale_chunk(image1, whole[ROUND - 1], True)
+        score_pixels(image1)
+        exponentiate(image1)
         burst_weights(image0)
         to_aggregate = list(range(CHUNKS))
 
@@ -670,18 +675,22 @@ def tile_salad_pa_k_kernel(tc, f_clu, h_score, W_s2, b_s2, burst_par, out):
             scale_chunk(image1, members[0], False)
             for k in range(2):
                 turn_step(rest0, on_scalar)
-            for k in range(2 if r > 0 else 0):
+            for k in range(A1 if r > 0 else 0):
                 similarity_pass()
                 aggregate_step()
             turn_back(image1, rescaled[r])
             scale_chunk(image1, members[1], False)
+            for k in range(NV0 if r > 0 else 0):
+                if to_aggregate:
+                    measure_aggregate(image0, to_aggregate[0])
+                    to_aggregate.remove(to_aggregate[0])
             if r + 1 < SS:
                 rescale_chunk(image1, rescaled[r + 1])
-            if r == 0:
-                weighted_assignment(image0)
-            for k in range(4 if r > 0 else 0):
+            for k in range(A2 if r > 0 else 0):
                 similarity_pass()
                 aggregate_step()
+            if r == 0:
+                weighted_assignment(image0)
             quantise_waiting()
             quantise_scaled(image1, rescaled[r])
             for c in members:
@@ -689,6 +698,7 @@ def tile_salad_pa_k_kernel(tc, f_clu, h_score, W_s2, b_s2, burst_par, out):
             if (r + 1) * ROUND < len(whole):
                 scale_chunk(image1, whole[(r + 2) * ROUND - 1], True)
         similarity_rest()
+        squares_from_stats(image0)
         cluster_norms(image0)
 
         burst_weights(image1)
@@ -697,7 +707,6 @@ def tile_salad_pa_k_kernel(tc, f_clu, h_score, W_s2, b_s2, burst_par, out):
             output_chunk(image0, c)
         weighted_assignment(image1)
         later = list(range(N1, CHUNKS))
-        image1["stats"] = small.tile([P, NV, 2, 3], F32, name="stats", tag="stats")
         for c in range(CHUNKS):
             if c % 3 == 2 and image1["measured_sums"] < NV:
                 measure_aggregate(image1, c)

@@ -24,21 +24,23 @@ CHUNKS = D_FEAT // K_PASS
 HALF = CHUNKS // 2
 EPS_NORM_SQUARED = 1e-24
 EPS_DENOM = 1e-6
-ROW_TILES = 21
+ROW_TILES = 22
 EARLY = 13
 SQUARED0 = 7
 TURNS_BEHIND = 1
 PARAMETERS_AT = 7
-HIDDEN_AT = 15
+HIDDEN_AT = 13
 EXP_AT = 3
 STEPS = 3
-VSTEP = (0, 0, 0, 1, 0)
+GRAM1 = 3
+STEPS0 = 2
+VSTEP = (0, 2, 2, 2, 4)
 SS = 4
-N1 = 9
+N1 = 7
 NV = 4
-NV0 = 2
-A1 = 2
-A2 = 3
+NV0 = 1
+A1 = 1
+A2 = 4
 ROUND = 3
 
 FLOPS = 2 * IMAGES * (K_CLU * F_HID * N_PIX + N_PIX * D_FEAT * N_PIX + D_FEAT * N_PIX * K_CLU)
@@ -49,7 +51,7 @@ def tile_salad_pa_k_kernel(tc, f_clu, h_score, W_s2, b_s2, burst_par, out):
     with ExitStack() as ctx:
         const = ctx.enter_context(tc.tile_pool(name="const", bufs=1))
         rows_pool = ctx.enter_context(tc.tile_pool(name="rows", bufs=ROW_TILES))
-        turned_pool = ctx.enter_context(tc.tile_pool(name="turned", bufs=6))
+        turned_pool = ctx.enter_context(tc.tile_pool(name="turned", bufs=5))
         image_pool = ctx.enter_context(tc.tile_pool(name="image", bufs=IMAGES))
         pass_pool = ctx.enter_context(tc.tile_pool(name="pass", bufs=3))
         codes_pool = ctx.enter_context(tc.tile_pool(name="codes", bufs=5))
@@ -523,7 +525,7 @@ def tile_salad_pa_k_kernel(tc, f_clu, h_score, W_s2, b_s2, burst_par, out):
 
         image0 = new_image(0)
         image1 = new_image(1)
-        for im, slots in ((image0, SQUARED0), (image1, CHUNKS)):
+        for im, slots in ((image0, SQUARED0), (image1, CHUNKS - GRAM1 + 1)):
             im["measured"] = 0
             im["pixel_squares"] = small.tile(
                 [P, PACK, slots], F32, name="pixel_squares", tag="pixel_squares%d" % im["index"]
@@ -563,7 +565,8 @@ def tile_salad_pa_k_kernel(tc, f_clu, h_score, W_s2, b_s2, burst_par, out):
         quantise_turned(image0, squared[-1])
 
         rest0 = [(image0, c) for c in others]
-        rest1 = [(image1, c) for c in range(CHUNKS)]
+        rest1 = [(image1, c) for c in range(GRAM1, CHUNKS)]
+        late1 = [(image1, c) for c in range(GRAM1)]
 
         waiting = []
         to_square = []
@@ -582,7 +585,7 @@ def tile_salad_pa_k_kernel(tc, f_clu, h_score, W_s2, b_s2, burst_par, out):
             empty_banks(im, c, copies)
             square_waiting()
             waiting.append((im, c))
-            if im is image1:
+            if im is image1 and c >= GRAM1:
                 to_square.append((im, c))
 
         def quantise_waiting(keep=0):
@@ -612,6 +615,7 @@ def tile_salad_pa_k_kernel(tc, f_clu, h_score, W_s2, b_s2, burst_par, out):
                 load_chunk(image1, len(image1["rows"]))
 
         order0 = squared + others
+        gram = [sim_banks.tile([P, P], F32, name="gram%d" % m, tag="sim") for m in range(PACK)]
         scale_chunk(image0, order0[ROUND - 1], True)
         for first in range(0, CHUNKS - 1, ROUND):
             for k in range(ROUND - 1):
@@ -620,23 +624,33 @@ def tile_salad_pa_k_kernel(tc, f_clu, h_score, W_s2, b_s2, burst_par, out):
                     score_pixels(image0)
                 if first == EXP_AT and k == 0:
                     exponentiate(image0)
+                load_next_chunk_of_image1()
                 for step in range(2):
-                    if 2 * k + step < STEPS:
+                    g = 2 * k + step
+                    if g < (STEPS0 if first == 0 else STEPS):
                         turn_step(rest1, on_scalar)
                         similarity_pass()
-            for c in range(ROUND):
-                load_next_chunk_of_image1()
-            source = (rest0, rest1)[VSTEP[first // ROUND]]
-            im, v = source[0]
-            source.remove(source[0])
-            transpose_chunk(im, v)
+                    if first == 0 and g < GRAM1:
+                        add_to_gram(gram, image1["rows"][g], g == 0, g == GRAM1 - 1)
+            load_next_chunk_of_image1()
+            kind = VSTEP[first // ROUND]
+            if kind == 0:
+                turn_step(rest0, on_scalar)
+            if kind == 1:
+                turn_step(late1, on_scalar)
+            if kind == 2 or kind == 3:
+                source = (rest0, late1)[kind - 2]
+                im, v = source[0]
+                source.remove(source[0])
+                transpose_chunk(im, v)
             quantise_waiting(TURNS_BEHIND)
             for k in range(ROUND):
                 quantise_scaled(image0, order0[first + k])
-            empty_banks(im, v, on_vector)
-            waiting.append((im, v))
-            if im is image1:
-                to_square.append((im, v))
+            if kind == 2 or kind == 3:
+                empty_banks(im, v, on_vector)
+                waiting.append((im, v))
+            if first == 0:
+                by_slot1 = reorder(diagonal_sums([block[:] for block in gram]), by_block, by_slot)
             if first + 2 * ROUND - 1 < CHUNKS:
                 scale_chunk(image0, order0[first + 2 * ROUND - 1], True)
         while rest1:
@@ -644,6 +658,7 @@ def tile_salad_pa_k_kernel(tc, f_clu, h_score, W_s2, b_s2, burst_par, out):
         square_waiting()
         scale_chunk(image0, order0[CHUNKS - 1], False)
         squared_norm1 = small.tile([P, PACK], F32, tag="squared_norm1")
+        nc.vector.tensor_copy(out=image1["pixel_squares"][:, :, CHUNKS - GRAM1], in_=by_slot1[:])
         sum_last(image1["pixel_squares"][:], squared_norm1[:])
         inverse_norm1 = inverse_root(squared_norm1, PACK)
         similarity_rest()
@@ -674,7 +689,7 @@ def tile_salad_pa_k_kernel(tc, f_clu, h_score, W_s2, b_s2, burst_par, out):
             members = whole[r * ROUND : (r + 1) * ROUND]
             scale_chunk(image1, members[0], False)
             for k in range(2):
-                turn_step(rest0, on_scalar)
+                turn_step(rest0 if rest0 else late1, on_scalar)
             for k in range(A1 if r > 0 else 0):
                 similarity_pass()
                 aggregate_step()
@@ -692,9 +707,9 @@ def tile_salad_pa_k_kernel(tc, f_clu, h_score, W_s2, b_s2, burst_par, out):
             if r == 0:
                 weighted_assignment(image0)
             quantise_waiting()
-            quantise_scaled(image1, rescaled[r])
             for c in members:
                 quantise_scaled(image1, c)
+            quantise_scaled(image1, rescaled[r])
             if (r + 1) * ROUND < len(whole):
                 scale_chunk(image1, whole[(r + 2) * ROUND - 1], True)
         similarity_rest()

@@ -707,9 +707,8 @@ def tile_salad_pa_k_kernel(tc, f_clu, h_score, W_s2, b_s2, burst_par, out):
             if r == 0:
                 weighted_assignment(image0)
             quantise_waiting()
-            for c in members:
+            for c in members[:2] + [rescaled[r]] + members[2:]:
                 quantise_scaled(image1, c)
-            quantise_scaled(image1, rescaled[r])
             if (r + 1) * ROUND < len(whole):
                 scale_chunk(image1, whole[(r + 2) * ROUND - 1], True)
         similarity_rest()

from contextlib import ExitStack

import concourse.mybir as mybir
from concourse.masks import make_identity

F32 = mybir.dt.float32
BF16 = mybir.dt.bfloat16
U32 = mybir.dt.uint32
U8 = mybir.dt.uint8
FP8X4 = mybir.dt.float8_e4m3fn_x4
ACT = mybir.ActivationFunctionType
ALU = mybir.AluOpType
AXIS = mybir.AxisListType

IMAGES = 2
D_FEAT = 8192
N_PIX = 512
K_CLU = 128
F_HID = 512
P = 128
PACK = 4
K_PASS = P * PACK
CHUNKS = D_FEAT // K_PASS
HALF = CHUNKS // 2
EPS_NORM_SQUARED = 1e-24
EPS_DENOM = 1e-6
ROW_TILES = 22
EARLY = 13
SQUARED0 = 7
TURNS_BEHIND = 1
PARAMETERS_AT = 7
HIDDEN_AT = 13
EXP_AT = 3
STEPS = 3
GRAM1 = 3
STEPS0 = 2
VSTEP = (0, 2, 2, 2, 4)
SS = 4
N1 = 7
NV = 4
NV0 = 1
A1 = 1
A2 = 4
ROUND = 3

FLOPS = 2 * IMAGES * (K_CLU * F_HID * N_PIX + N_PIX * D_FEAT * N_PIX + D_FEAT * N_PIX * K_CLU)


def tile_salad_pa_k_kernel(tc, f_clu, h_score, W_s2, b_s2, burst_par, out):
    nc = tc.nc
    with ExitStack() as ctx:
        const = ctx.enter_context(tc.tile_pool(name="const", bufs=1))
        rows_pool = ctx.enter_context(tc.tile_pool(name="rows", bufs=ROW_TILES))
        turned_pool = ctx.enter_context(tc.tile_pool(name="turned", bufs=5))
        image_pool = ctx.enter_context(tc.tile_pool(name="image", bufs=IMAGES))
        pass_pool = ctx.enter_context(tc.tile_pool(name="pass", bufs=3))
        codes_pool = ctx.enter_context(tc.tile_pool(name="codes", bufs=5))
        gpsimd_pool = ctx.enter_context(tc.tile_pool(name="gpsimd", bufs=1))
        unread_pool = ctx.enter_context(tc.tile_pool(name="unread", bufs=2))
        small = ctx.enter_context(tc.tile_pool(name="small", bufs=2))
        sim_banks = ctx.enter_context(tc.psum_pool(name="sim_banks", bufs=PACK))
        norm_bank = ctx.enter_context(tc.psum_pool(name="norm_bank", bufs=1))
        banks = ctx.enter_context(tc.psum_pool(name="banks", bufs=3))

        ctx.enter_context(tc.manual_schedule())

        ident = const.tile([P, P], F32)
        make_identity(nc, ident[:])
        first_exp = const.tile([P, 1], F32)
        nc.vector.memset(first_exp[:], 0.0)
        nc.scalar.activation(out=first_exp[:], in_=first_exp[:], func=ACT.Exp)

        w_rows = const.tile([K_CLU, F_HID], BF16)
        nc.scalar.dma_start(out=w_rows[:], in_=W_s2)
        row = const.tile([P, K_CLU + PACK], BF16)
        nc.vector.memset(row[:], 0.0)
        nc.scalar.dma_start(out=row[0:1, 0:K_CLU], in_=b_s2.unsqueeze(0))
        nc.scalar.dma_start(out=row[0:1, K_CLU : K_CLU + 3], in_=burst_par.unsqueeze(0))
        ones = const.tile([P, P], BF16)
        nc.vector.memset(ones[:], 1.0)
        minus_half = const.tile([P, PACK], F32)
        nc.vector.memset(minus_half[:], -0.5)

        def load_rows(dram_rows):
            rows = rows_pool.tile([P, PACK, N_PIX], BF16, tag="rows", align_bytes=64)
            nc.sync.dma_start(out=rows[:], in_=dram_rows.rearrange("(p j) n -> p j n", j=PACK))
            return rows

        def columns_by_slot(grouped):
            return grouped[:].rearrange("p (t q) j -> p q j t", t=PACK)

        def pixels_by_slot(rows):
            return rows[:].rearrange("p j (q t) -> p q j t", t=PACK)

        def quantise(grouped_columns, codes, scales):
            nc.vector.quantize_mx(
                out=codes.bitcast(FP8X4),
                scales=scales,
                in_=grouped_columns.rearrange("p c j -> p (c j)"),
            )

        def quantise_pass(grouped):
            codes = codes_pool.tile([P, N_PIX], U32, tag="codes", align_bytes=64)
            scales = codes_pool.tile([P, N_PIX], U8, tag="scales", align_bytes=64)
            quantise(grouped[:], codes[:], scales[:])
            return codes, scales

        def inverse_root(squares, width):
            floored = small.tile([P, width], F32, tag="floored%d" % width)
            nc.vector.tensor_scalar_max(out=floored[:], in0=squares[:], scalar1=EPS_NORM_SQUARED)
            inverse = small.tile([P, width], F32, tag="inverse%d" % width)
            nc.gpsimd.tensor_tensor(
                out=inverse[:], in0=floored[:], in1=minus_half[:, 0:width], op=ALU.pow
            )
            return inverse

        def spread_over_partitions(bank_views, per_partition):
            for k, view in enumerate(bank_views):
                nc.tensor.transpose(view, per_partition[:, k : k + 1].to_broadcast([P, P]), ident[:])

        def fetch_parameters():
            spread_row = banks.tile([P, K_CLU + PACK], F32, name="spread_row", tag="bank")
            nc.tensor.matmul(out=spread_row[:], lhsT=ones[:], rhs=row[:], start=True, stop=True)
            held = const.tile([P, K_CLU + PACK], F32, name="held")
            nc.vector.tensor_copy(out=held[:], in_=spread_row[:])
            exponent = const.tile([P, PACK], F32, name="exponent")
            nc.vector.tensor_copy(
                out=exponent[:], in_=held[:, K_CLU + 2 : K_CLU + 3].to_broadcast([P, PACK])
            )
            return held, exponent

        def quantise_w():
            w_words = w_rows[:].bitcast(F32).rearrange("k (q u) -> k u q", u=2)
            w_turned = banks.tile([P, 2, K_CLU], F32, name="w_turned", tag="bank")
            for u in range(2):
                nc.tensor.transpose(w_turned[:, u, :], w_words[:, u, :], ident[:])
            w_grouped = const.tile([P, K_CLU, PACK], BF16, name="w_grouped", align_bytes=64)
            nc.vector.tensor_copy(
                out=w_grouped[:].bitcast(F32), in_=w_turned[:].rearrange("q u k -> q k u")
            )
            w_codes = const.tile([P, K_CLU], U32, name="w_codes", align_bytes=64)
            w_scales = const.tile([P, K_CLU], U8, name="w_scales", align_bytes=64)
            quantise(w_grouped[:], w_codes[:], w_scales[:])
            return w_codes, w_scales

        def new_image(i):
            return {
                "index": i,
                "rows": [],
                "banks": {},
                "turned": {},
                "scaled": {},
                "fT_codes": image_pool.tile(
                    [P, D_FEAT], U32, name="fT_codes", tag="fT_codes", align_bytes=64
                ),
                "fT_scales": image_pool.tile(
                    [P, D_FEAT], U8, name="fT_scales", tag="fT_scales", align_bytes=64
                ),
                "cluster_squares": small.tile(
                    [P, 2 * CHUNKS], F32, name="cluster_squares", tag="cluster_squares"
                ),
                "sums": 0,
                "measured_sums": 0,
                "stats": small.tile([P, CHUNKS // 2, 2, 3], F32, name="stats", tag="stats"),
            }

        def load_chunk(im, c):
            im["rows"].append(load_rows(f_clu[im["index"], c * K_PASS : (c + 1) * K_PASS, :]))

        def transpose_chunk(im, c, pools=None):
            words = im["rows"][c][:].bitcast(F32).rearrange("p j (q u) -> p j u q", u=2)
            im["banks"][c] = []
            for half in range(2):
                pool, tag = (banks, "bank") if pools is None else pools[half]
                bank = pool.tile([P, 2, 2, P], F32, name="turned_bank", tag=tag)
                for jj in range(2):
                    for u in range(2):
                        nc.tensor.transpose(bank[:, jj, u, :], words[:, 2 * half + jj, u, :], ident[:])
                im["banks"][c].append(bank)

        def empty_banks(im, c, copies):
            turned = turned_pool.tile([P, K_PASS, PACK], BF16, name="turned", tag="turned", align_bytes=64)
            turned_words = turned[:].bitcast(F32)
            for half in range(2):
                first = half * 2 * P
                copies[half](
                    out=turned_words[:, first : first + 2 * P, :].rearrange(
                        "q (jj p) u -> q jj p u", jj=2
                    ),
                    in_=im["banks"][c][half][:].rearrange("q jj u p -> q jj p u"),
                )
            im["turned"][c] = turned

        def quantise_turned(im, c):
            columns = slice(c * K_PASS, (c + 1) * K_PASS)
            quantise(im["turned"][c][:], im["fT_codes"][:, columns], im["fT_scales"][:, columns])

        def square_chunk(im, c):
            for t in range(PACK):
                unread = unread_pool.tile([P, K_PASS], BF16, tag="bank_wide")
                nc.scalar.activation(
                    out=unread[:],
                    in_=im["turned"][c][:, :, t],
                    func=ACT.Square,
                    accum_out=im["pixel_squares"][:, t, im["measured"] : im["measured"] + 1],
                )
            im["measured"] += 1

        def load_hidden(im):
            im["h_rows"] = load_rows(h_score[im["index"]])

        def quantise_hidden(im):
            h_grouped = pass_pool.tile([P, N_PIX, PACK], BF16, tag="grouped", align_bytes=64)
            nc.vector.tensor_copy(out=columns_by_slot(h_grouped), in_=pixels_by_slot(im["h_rows"]))
            im["h"] = quantise_pass(h_grouped)

        def score_pixels(im):
            h_codes, h_scales = im["h"]
            product = banks.tile([P, PACK, K_CLU], F32, name="product", tag="bank")
            for t in range(PACK):
                nc.tensor.matmul_mx(
                    out=product[:, t, :],
                    lhsT=h_codes[:, t * P : (t + 1) * P].bitcast(FP8X4),
                    lhsT_scale=h_scales[:, t * P : (t + 1) * P],
                    rhs=w_codes[:].bitcast(FP8X4),
                    rhs_scale=w_scales[:],
                    start=True,
                    stop=True,
                )
            im["expo"] = image_pool.tile([P, PACK, K_CLU], F32, name="expo", tag="expo")
            nc.vector.scalar_tensor_tensor(
                out=im["expo"][:],
                in0=product[:],
                scalar=-1.0,
                in1=held[:, 0:K_CLU].unsqueeze(1).to_broadcast([P, PACK, K_CLU]),
                op0=ALU.mult,
                op1=ALU.subtract,
            )
            im["least"] = small.tile([P, PACK], F32, name="least", tag="least")
            nc.vector.tensor_reduce(
                out=im["least"][:], in_=im["expo"][:], axis=AXIS.X, op=ALU.min
            )

        def exponentiate(im):
            im["expo_sum"] = image_pool.tile([P, PACK], F32, name="expo_sum", tag="expo_sum")
            for t in range(PACK):
                nc.scalar.activation(
                    out=im["expo"][:, t, :],
                    in_=im["expo"][:, t, :],
                    func=ACT.Exp,
                    scale=-1.0,
                    bias=im["least"][:, t : t + 1],
                    accum_out=im["expo_sum"][:, t : t + 1],
                )

        def add_to_gram(gram, rows, first, last):
            for j in range(PACK):
                for m in range(PACK):
                    block = rows[:, j, m * P : (m + 1) * P]
                    nc.tensor.matmul(
                        out=gram[m][:],
                        lhsT=block,
                        rhs=block,
                        start=(first and j == 0),
                        stop=(last and j == PACK - 1),
                    )

        def diagonal_sums(blocks):
            sums = small.tile([P, PACK], F32, name="diagonal_sums", tag="diagonal_sums")
            for m in range(PACK):
                unread = unread_pool.tile([P, P], F32, name="unread", tag="masked")
                nc.vector.scalar_tensor_tensor(
                    out=unread[:],
                    in0=blocks[m],
                    scalar=1.0,
                    in1=ident[:],
                    op0=ALU.mult,
                    op1=ALU.mult,
                    accum_out=sums[:, m : m + 1],
                )
            return sums

        def by_block(bank):
            return bank[:].rearrange("p (m i) -> p m i", m=PACK)

        def by_slot(bank):
            return bank[:].rearrange("p (q t) -> p t q", t=PACK)

        def reorder(per_pixel, source, target):
            spread = banks.tile([P, N_PIX], F32, name="reorder_bank", tag="bank")
            spread_over_partitions([source(spread)[:, k, :] for k in range(PACK)], per_pixel)
            return diagonal_sums([target(spread)[:, k, :] for k in range(PACK)])

        def sum_last(values, out):
            nc.vector.tensor_reduce(out=out, in_=values, axis=AXIS.X, op=ALU.add)

        def spread_pixel_norms(im, inverse_norm, order):
            spread = norm_bank.tile([P, N_PIX], F32, tag="spread")
            spread_over_partitions([order(spread)[:, k, :] for k in range(PACK)], inverse_norm)
            im["spread"] = spread

        def copy_pixel_norms(im):
            spread_copy = const.tile([P, N_PIX], F32, tag="spread_copy")
            nc.vector.tensor_copy(out=spread_copy[:], in_=im["spread"][:])
            im["spread_copy"] = spread_copy

        def scale_chunk(im, c, on_gpsimd):
            if on_gpsimd:
                grouped = gpsimd_pool.tile([P, N_PIX, PACK], BF16, tag="grouped", align_bytes=64)
                engine, norms = nc.gpsimd, im["spread_copy"]
            else:
                grouped = pass_pool.tile([P, N_PIX, PACK], BF16, tag="grouped", align_bytes=64)
                engine, norms = nc.vector, im["spread"]
            engine.tensor_tensor(
                out=columns_by_slot(grouped),
                in0=pixels_by_slot(im["rows"][c]),
                in1=norms[:]
                .rearrange("p (q t) -> p q t", t=PACK)
                .unsqueeze(2)
                .to_broadcast([P, P, PACK, PACK]),
                op=ALU.mult,
            )
            im["scaled"][c] = grouped

        def rescale_chunk(im, c):
            scaled = rows_pool.tile([P, PACK, K_PASS], BF16, tag="rows", align_bytes=64)
            for t in range(PACK):
                nc.scalar.activation(
                    out=scaled[:, t, :].rearrange("q (v p e) -> q v p e", v=2, e=2),
                    in_=im["turned"][c][:, :, t].rearrange("q (v e p) -> q v p e", v=2, e=2),
                    func=ACT.Copy,
                    scale=im["inverse_norm"][:, t : t + 1],
                )
            im["rescaled"] = scaled

        def turn_back(im, c):
            words = im["rescaled"][:].bitcast(F32)
            grouped = rows_pool.tile([P, N_PIX, PACK], BF16, tag="rows", align_bytes=64)
            grouped_words = grouped[:].bitcast(F32)
            for half in range(2):
                bank = banks.tile([P, 2, 2, P], F32, name="turned_bank", tag="bank")
                for tt in range(2):
                    for v in range(2):
                        nc.tensor.transpose(
                            bank[:, tt, v, :], words[:, 2 * half + tt, v * P : (v + 1) * P], ident[:]
                        )
                nc.scalar.copy(
                    out=grouped_words[:, half * 2 * P : (half + 1) * 2 * P, :].rearrange(
                        "p (tt q) v -> p tt q v", tt=2
                    ),
                    in_=bank[:].rearrange("p tt v q -> p tt q v"),
                )
            im["scaled"][c] = grouped

        passes = []
        quantised = []

        def quantise_scaled(im, c):
            quantised.append((im, c, quantise_pass(im["scaled"][c])))

        def similarity_pass():
            if not quantised:
                return
            im, c, (fn_codes, fn_scales) = quantised[0]
            quantised.remove(quantised[0])
            n = len(passes) % CHUNKS
            passes.append(c)
            if n == 0:
                im["sim"] = [
                    sim_banks.tile([P, N_PIX], F32, name="sim%d" % t, tag="sim") for t in range(PACK)
                ]
            for t in range(PACK):
                nc.tensor.matmul_mx(
                    out=im["sim"][t][:],
                    lhsT=fn_codes[:, t * P : (t + 1) * P].bitcast(FP8X4),
                    lhsT_scale=fn_scales[:, t * P : (t + 1) * P],
                    rhs=fn_codes[:].bitcast(FP8X4),
                    rhs_scale=fn_scales[:],
                    start=(n == 0),
                    stop=(n == CHUNKS - 1),
                )

        def similarity_rest():
            while quantised:
                similarity_pass()

        def burst_weights(im):
            w = small.tile([P, PACK], F32, tag="w")
            for t in range(PACK):
                unread = unread_pool.tile([P, N_PIX], BF16, tag="bank_wide")
                nc.scalar.activation(
                    out=unread[:],
                    in_=im["sim"][t][:],
                    func=ACT.Sigmoid,
                    scale=held[:, K_CLU : K_CLU + 1],
                    bias=held[:, K_CLU + 1 : K_CLU + 2],
                    accum_out=w[:, t : t + 1],
                )
            w_power = small.tile([P, PACK], F32, tag="w_power")
            nc.gpsimd.tensor_tensor(out=w_power[:], in0=w[:], in1=exponent[:], op=ALU.pow)
            im["w_power"] = w_power

        def weighted_assignment(im):
            divisor = small.tile([P, PACK], F32, tag="divisor")
            nc.vector.scalar_tensor_tensor(
                out=divisor[:],
                in0=im["w_power"][:],
                scalar=EPS_DENOM,
                in1=im["expo_sum"][:],
                op0=ALU.add,
                op1=ALU.mult,
            )
            share = small.tile([P, PACK], F32, tag="share")
            nc.vector.reciprocal(out=share[:], in_=divisor[:])
            pm_grouped = small.tile([P, K_CLU, PACK], BF16, tag="pm_grouped", align_bytes=64)
            nc.vector.tensor_tensor(
                out=pm_grouped[:],
                in0=im["expo"][:].rearrange("q t k -> q k t"),
                in1=share[:].unsqueeze(1).to_broadcast([P, K_CLU, PACK]),
                op=ALU.mult,
            )
            pm_codes = image_pool.tile([P, K_CLU], U32, tag="pm_codes", align_bytes=64)
            pm_scales = image_pool.tile([P, K_CLU], U8, tag="pm_scales", align_bytes=64)
            quantise(pm_grouped[:], pm_codes[:], pm_scales[:])
            im["pm_codes"] = pm_codes
            im["pm_scales"] = pm_scales

        def turned_aggregate(im, c):
            columns = slice(c * K_PASS, (c + 1) * K_PASS)
            pool, tag = (banks, "bank") if im["index"] == 0 else (sim_banks, "sim")
            v_turned = pool.tile([P, K_PASS], F32, name="v_turned", tag=tag)
            nc.tensor.matmul_mx(
                out=v_turned[:],
                lhsT=im["pm_codes"][:].bitcast(FP8X4),
                lhsT_scale=im["pm_scales"][:],
                rhs=im["fT_codes"][:, columns].bitcast(FP8X4),
                rhs_scale=im["fT_scales"][:, columns],
                start=True,
                stop=True,
            )
            return v_turned

        def square_aggregate(im, c):
            v_turned = turned_aggregate(im, c)
            unread = unread_pool.tile([P, K_PASS], BF16, tag="bank_wide")
            n = im["sums"]
            nc.scalar.activation(
                out=unread[:],
                in_=v_turned[:],
                func=ACT.Square,
                accum_out=im["cluster_squares"][:, n : n + 1],
            )
            im["sums"] += 1

        def measure_aggregate(im, c):
            v_turned = turned_aggregate(im, c)
            n = im["measured_sums"]
            nc.vector.bn_stats(
                out=im["stats"][:, n, :, :].rearrange("p h s -> p (h s)"), in_=v_turned[:]
            )
            im["measured_sums"] += 1

        def squares_from_stats(im):
            n, first = im["measured_sums"], im["sums"]
            stats = im["stats"][:, 0:n, :, :].rearrange("p n h s -> p (n h) s")
            mean_squared = small.tile([P, 2 * n], F32, name="mean_squared", tag="mean_squared")
            nc.vector.scalar_tensor_tensor(
                out=mean_squared[:],
                in0=stats[:, :, 1],
                scalar=float(K_PASS // 2),
                in1=stats[:, :, 1],
                op0=ALU.mult,
                op1=ALU.mult,
            )
            nc.vector.tensor_tensor(
                out=im["cluster_squares"][:, first : first + 2 * n],
                in0=mean_squared[:],
                in1=stats[:, :, 2],
                op=ALU.add,
            )
            im["sums"] += 2 * n

        def cluster_norms(im):
            squared_norm = small.tile([P, 1], F32, tag="v_squared_norm")
            nc.vector.tensor_reduce(
                out=squared_norm[:], in_=im["cluster_squares"][:, 0 : im["sums"]], axis=AXIS.X, op=ALU.add
            )
            inverse_norm = inverse_root(squared_norm, 1)
            spread_bank = banks.tile([P, K_CLU], F32, tag="bank")
            spread_over_partitions([spread_bank[:]], inverse_norm)
            im["v_spread_bank"] = spread_bank

        def fetch_cluster_norms(im):
            v_spread = small.tile([P, K_CLU], F32, tag="v_spread")
            nc.vector.tensor_copy(out=v_spread[:], in_=im["v_spread_bank"][:])
            im["v_spread"] = v_spread

        def output_chunk(im, c):
            pool, tag = (banks, "bank") if im["index"] == 0 or c % 2 == 0 else (sim_banks, "sim")
            v = pool.tile([P, PACK, K_CLU], F32, name="v", tag=tag)
            for j in range(PACK):
                columns = slice(c * K_PASS + j * P, c * K_PASS + (j + 1) * P)
                nc.tensor.matmul_mx(
                    out=v[:, j, :],
                    lhsT=im["fT_codes"][:, columns].bitcast(FP8X4),
                    lhsT_scale=im["fT_scales"][:, columns],
                    rhs=im["pm_codes"][:].bitcast(FP8X4),
                    rhs_scale=im["pm_scales"][:],
                    start=True,
                    stop=True,
                )
            normed = rows_pool.tile([P, PACK, K_CLU], F32, tag="rows", align_bytes=64)
            nc.vector.tensor_tensor(
                out=normed[:],
                in0=v[:],
                in1=im["v_spread"][:].unsqueeze(1).to_broadcast([P, PACK, K_CLU]),
                op=ALU.mult,
            )
            nc.sync.dma_start(
                out=out[im["index"], c * K_PASS : (c + 1) * K_PASS, :].rearrange(
                    "(p j) k -> p j k", j=PACK
                ),
                in_=normed[:],
            )

        image0 = new_image(0)
        image1 = new_image(1)
        for im, slots in ((image0, SQUARED0), (image1, CHUNKS - GRAM1 + 1)):
            im["measured"] = 0
            im["pixel_squares"] = small.tile(
                [P, PACK, slots], F32, name="pixel_squares", tag="pixel_squares%d" % im["index"]
            )

        for c in range(EARLY):
            load_chunk(image0, c)
        load_hidden(image0)
        for c in range(EARLY, CHUNKS):
            load_chunk(image0, c)
        load_hidden(image1)
        for c in range(ROW_TILES - CHUNKS - IMAGES):
            load_chunk(image1, c)

        on_scalar = (nc.scalar.copy, nc.scalar.copy)
        on_vector = (nc.vector.tensor_copy, nc.vector.tensor_copy)
        on_both = (nc.scalar.copy, nc.vector.tensor_copy)

        gram = [sim_banks.tile([P, P], F32, name="gram%d" % m, tag="sim") for m in range(PACK)]
        squared = [0] + [2 * k + 1 for k in range(SQUARED0 - 1)]
        others = [c for c in range(CHUNKS) if c not in squared]
        for c in range(CHUNKS):
            if c in squared:
                transpose_chunk(image0, c)
                empty_banks(image0, c, on_vector)
                square_chunk(image0, c)
                if c > 0:
                    quantise_turned(image0, squared[squared.index(c) - 1])
            else:
                add_to_gram(gram, image0["rows"][c], c == others[0], c == others[-1])
            if c == PARAMETERS_AT:
                held, exponent = fetch_parameters()
                w_codes, w_scales = quantise_w()
            if c == HIDDEN_AT:
                quantise_hidden(image0)
                load_chunk(image1, len(image1["rows"]))
        quantise_turned(image0, squared[-1])

        rest0 = [(image0, c) for c in others]
        rest1 = [(image1, c) for c in range(GRAM1, CHUNKS)]
        late1 = [(image1, c) for c in range(GRAM1)]

        waiting = []
        to_square = []

        def square_waiting():
            for im, c in to_square:
                square_chunk(im, c)
            to_square.clear()

        def turn_step(rest, copies):
            if not rest:
                return
            im, c = rest[0]
            rest.remove(rest[0])
            transpose_chunk(im, c)
            empty_banks(im, c, copies)
            square_waiting()
            waiting.append((im, c))
            if im is image1 and c >= GRAM1:
                to_square.append((im, c))

        def quantise_waiting(keep=0):
            while len(waiting) > keep:
                im, c = waiting[0]
                waiting.remove(waiting[0])
                quantise_turned(im, c)

        partial = small.tile([P, PACK], F32, tag="partial")
        sum_last(image0["pixel_squares"][:], partial[:])
        partial_by_block = reorder(partial, by_slot, by_block)
        turn_step(rest0, on_scalar)
        turn_step(rest0, on_scalar)
        squared_norm0 = small.tile([P, PACK], F32, tag="squared_norm0")
        nc.vector.tensor_tensor(
            out=squared_norm0[:],
            in0=diagonal_sums([block[:] for block in gram])[:],
            in1=partial_by_block[:],
            op=ALU.add,
        )
        inverse_norm0 = inverse_root(squared_norm0, PACK)
        spread_pixel_norms(image0, inverse_norm0, by_block)
        copy_pixel_norms(image0)

        def load_next_chunk_of_image1():
            if len(image1["rows"]) < CHUNKS:
                load_chunk(image1, len(image1["rows"]))

        order0 = squared + others
        gram = [sim_banks.tile([P, P], F32, name="gram%d" % m, tag="sim") for m in range(PACK)]
        scale_chunk(image0, order0[ROUND - 1], True)
        for first in range(0, CHUNKS - 1, ROUND):
            for k in range(ROUND - 1):
                scale_chunk(image0, order0[first + k], False)
                if first == 0 and k == 0:
                    score_pixels(image0)
                if first == EXP_AT and k == 0:
                    exponentiate(image0)
                load_next_chunk_of_image1()
                for step in range(2):
                    g = 2 * k + step
                    if g < (STEPS0 if first == 0 else STEPS):
                        turn_step(rest1, on_scalar)
                        similarity_pass()
                    if first == 0 and g < GRAM1:
                        add_to_gram(gram, image1["rows"][g], g == 0, g == GRAM1 - 1)
            load_next_chunk_of_image1()
            kind = VSTEP[first // ROUND]
            if kind == 0:
                turn_step(rest0, on_scalar)
            if kind == 1:
                turn_step(late1, on_scalar)
            if kind == 2 or kind == 3:
                source = (rest0, late1)[kind - 2]
                im, v = source[0]
                source.remove(source[0])
                transpose_chunk(im, v)
            quantise_waiting(TURNS_BEHIND)
            for k in range(ROUND):
                quantise_scaled(image0, order0[first + k])
            if kind == 2 or kind == 3:
                empty_banks(im, v, on_vector)
                waiting.append((im, v))
            if first == 0:
                by_slot1 = reorder(diagonal_sums([block[:] for block in gram]), by_block, by_slot)
            if first + 2 * ROUND - 1 < CHUNKS:
                scale_chunk(image0, order0[first + 2 * ROUND - 1], True)
        while rest1:
            turn_step(rest1, on_scalar)
        square_waiting()
        scale_chunk(image0, order0[CHUNKS - 1], False)
        squared_norm1 = small.tile([P, PACK], F32, tag="squared_norm1")
        nc.vector.tensor_copy(out=image1["pixel_squares"][:, :, CHUNKS - GRAM1], in_=by_slot1[:])
        sum_last(image1["pixel_squares"][:], squared_norm1[:])
        inverse_norm1 = inverse_root(squared_norm1, PACK)
        similarity_rest()
        quantise_waiting()
        quantise_scaled(image0, order0[CHUNKS - 1])
        similarity_rest()
        image1["inverse_norm"] = inverse_norm1
        whole = list(range(CHUNKS - SS))
        rescaled = list(range(CHUNKS - SS, CHUNKS))
        rescale_chunk(image1, rescaled[0])
        quantise_hidden(image1)
        spread_pixel_norms(image1, inverse_norm1, by_slot)
        copy_pixel_norms(image1)

        scale_chunk(image1, whole[ROUND - 1], True)
        score_pixels(image1)
        exponentiate(image1)
        burst_weights(image0)
        to_aggregate = list(range(CHUNKS))

        def aggregate_step():
            if to_aggregate:
                square_aggregate(image0, to_aggregate[0])
                to_aggregate.remove(to_aggregate[0])

        rounds = len(whole) // ROUND
        for r in range(rounds):
            members = whole[r * ROUND : (r + 1) * ROUND]
            scale_chunk(image1, members[0], False)
            for k in range(2):
                turn_step(rest0 if rest0 else late1, on_scalar)
            for k in range(A1 if r > 0 else 0):
                similarity_pass()
                aggregate_step()
            turn_back(image1, rescaled[r])
            scale_chunk(image1, members[1], False)
            for k in range(NV0 if r > 0 else 0):
                if to_aggregate:
                    measure_aggregate(image0, to_aggregate[0])
                    to_aggregate.remove(to_aggregate[0])
            if r + 1 < SS:
                rescale_chunk(image1, rescaled[r + 1])
            for k in range(A2 if r > 0 else 0):
                similarity_pass()
                aggregate_step()
            if r == 0:
                weighted_assignment(image0)
            quantise_waiting()
            for c in members[:2] + [rescaled[r]] + members[2:]:
                quantise_scaled(image1, c)
            if (r + 1) * ROUND < len(whole):
                scale_chunk(image1, whole[(r + 2) * ROUND - 1], True)
        similarity_rest()
        squares_from_stats(image0)
        cluster_norms(image0)

        burst_weights(image1)
        fetch_cluster_norms(image0)
        for c in range(N1):
            output_chunk(image0, c)
        weighted_assignment(image1)
        later = list(range(N1, CHUNKS))
        for c in range(CHUNKS):
            if c % 3 == 2 and image1["measured_sums"] < NV:
                measure_aggregate(image1, c)
            else:
                square_aggregate(image1, c)
                if later and c % 2 == 0:
                    output_chunk(image0, later[0])
                    later.remove(later[0])
        squares_from_stats(image1)
        for c in later:
            output_chunk(image0, c)
        cluster_norms(image1)
        fetch_cluster_norms(image1)
        for c in range(CHUNKS):
            output_chunk(image1, c)
